import numpy as np
import ml_dtypes


def mxq(x, axis, fmt="e4m3"):
    dtype, down = {"e4m3": (ml_dtypes.float8_e4m3fn, 7), "e5m2": (ml_dtypes.float8_e5m2, 14)}[fmt]
    v = np.moveaxis(np.asarray(x, np.float32).astype(ml_dtypes.bfloat16).astype(np.float64), axis, -1)
    blocks = v.reshape(v.shape[:-1] + (-1, 32))
    amax = np.abs(blocks).max(-1, keepdims=True)
    byte = np.maximum(np.where(amax > 0, np.frexp(amax)[1] - 1 + 127, 0) - down, 1)
    scale = np.exp2(byte - 127.0)
    codes = (blocks / scale).astype(np.float32).astype(dtype).astype(np.float64)
    return np.moveaxis((codes * scale).reshape(v.shape), -1, axis)


WIDE = False


def mx_kscale(k):
    if not WIDE:
        return np.ones(k)
    levels = np.array([10, -10, 5, -5, 0])
    if k % 512:
        return np.exp2(np.random.permutation(np.resize(levels, k // 32))).repeat(32)
    a = np.empty((k // 512, 16))
    for p in range(k // 512):
        a[p, :8] = np.random.permutation(np.resize(levels, 8))
        for g in range(8):
            far = levels[np.abs(levels - a[p, g]) >= 10]
            a[p, g + 8] = far[np.random.randint(len(far))]
    return np.exp2(a.ravel()).repeat(32)


BF16 = ml_dtypes.bfloat16


def bf(x):
    return np.asarray(x, np.float32).astype(BF16)


def f64(x):
    return np.asarray(x).astype(np.float64)


B, CK, CV, NOBJ, T, H, W = 1, 128, 256, 2, 64, 16, 16
N = T * H * W
P = H * W
V = NOBJ * CV


def setup_inputs():
    s = mx_kscale(N)
    a = np.log2(s) - np.log2(s).min()
    g = np.exp2(np.round(np.log2(np.mean(1.0 / s))))
    ms = bf(1.0 + 0.5 * np.random.random((B, T, H, W)))[:, None]
    qe = np.random.random((B, CK, H, W))
    qe[:, 0] = 1.0
    m2 = np.random.standard_normal((B, CK, T, H, W)) ** 2
    m2[:, 0] += (a * np.log(2.0) * np.sqrt(CK)).reshape(T, H, W) / f64(ms)[:, 0]
    return {
        "query_key": bf(np.random.standard_normal((B, CK, H, W))),
        "query_selection": bf(qe),
        "qk_sel": bf(np.random.standard_normal((B, CK, H, W)) * np.random.random((B, CK, H, W))),
        "memory_key": bf(np.random.standard_normal((B, CK, T, H, W))),
        "mk_sq": bf(m2),
        "memory_shrinkage": ms,
        "memory_value": bf(2.0 * np.random.standard_normal((B, NOBJ, CV, T, H, W)) * (s * g).reshape(T, H, W)),
    }


def reference(query_key, query_selection, qk_sel, memory_key, mk_sq, memory_shrinkage, memory_value):
    qk = f64(query_key).reshape(B, CK, P)
    qe = f64(query_selection).reshape(B, CK, P)
    qs = f64(qk_sel).reshape(B, CK, P)
    mk = f64(memory_key).reshape(B, CK, N)
    m2 = f64(mk_sq).reshape(B, CK, N)
    ms = f64(memory_shrinkage).reshape(B, N)
    mv = f64(memory_value).reshape(B, V, N)
    a_sq = m2.transpose(0, 2, 1) @ qe
    two_ab = 2.0 * (mk.transpose(0, 2, 1) @ qs)
    b_sq = np.sum(qe * qk * qk, axis=1, keepdims=True)
    sim = (two_ab - a_sq - b_sq) * ms[:, :, None] * (1.0 / np.sqrt(CK))
    e = np.exp(sim - sim.max(axis=1, keepdims=True))
    mem = (mxq(mv, 2, "e4m3") @ mxq(e, 1, "e4m3")) / e.sum(axis=1, keepdims=True)
    return mem.reshape(B, NOBJ, CV, H, W)

@@ -1,0 +1,348 @@
+import math
+from contextlib import ExitStack
+
+import concourse.mybir as mybir
+from concourse.masks import make_identity
+
+F32 = mybir.dt.float32
+BF16 = mybir.dt.bfloat16
+U32 = mybir.dt.uint32
+U8 = mybir.dt.uint8
+FP8X4 = mybir.dt.float8_e4m3fn_x4
+ALU = mybir.AluOpType
+ACT = mybir.ActivationFunctionType
+AXIS = mybir.AxisListType
+
+P = 128
+CK = 128
+PIX = 256
+PIX_TILES = PIX // P
+SLOTS = 16384
+VAL = 512
+VAL_TILES = VAL // P
+HALF_VAL = VAL // 2
+K_PASS = 4 * P
+PASSES = SLOTS // K_PASS
+CHUNK = 2048
+CHUNKS = SLOTS // CHUNK
+PASSES_PER_CHUNK = CHUNK // K_PASS
+PAIR = 2 * K_PASS
+PAIRS = SLOTS // PAIR
+PAIRS_PER_CHUNK = CHUNK // PAIR
+INV_SQRT_CK = 1.0 / math.sqrt(CK)
+
+FLOPS = 2 * SLOTS * PIX * (2 * CK + VAL)
+
+
+def tile_xmem_pa_k_kernel(
+    tc,
+    query_key,
+    query_selection,
+    qk_sel,
+    memory_key,
+    mk_sq,
+    memory_shrinkage,
+    memory_value,
+    out,
+):
+    nc = tc.nc
+
+    qk_dram = query_key.rearrange("b c h w -> (b c) (h w)")
+    qe_dram = query_selection.rearrange("b c h w -> (b c) (h w)")
+    qs_dram = qk_sel.rearrange("b c h w -> (b c) (h w)")
+    mk_dram = memory_key.rearrange("b c t h w -> (b c) (t h w)")
+    m2_dram = mk_sq.rearrange("b c t h w -> (b c) (t h w)")
+    ms_dram = memory_shrinkage.rearrange("b o t h w -> (b o t h w)")
+    mv_dram = memory_value.rearrange("b o c t h w -> (b o c) (t h w)").rearrange(
+        "(q r) n -> r q n", r=P
+    )
+    out_dram = out.rearrange("b o c h w -> (b o c) (h w)").rearrange("(q r) p -> r q p", r=P)
+
+    with ExitStack() as whole:
+        const = whole.enter_context(tc.tile_pool(name="const", bufs=1))
+        sim_pool = whole.enter_context(tc.tile_pool(name="sim", bufs=1))
+        early_pool = whole.enter_context(tc.tile_pool(name="early", bufs=1))
+        raw_pool = whole.enter_context(tc.tile_pool(name="raw", bufs=4))
+        grouped_pool = whole.enter_context(tc.tile_pool(name="grouped", bufs=3))
+        psum_val = whole.enter_context(tc.psum_pool(name="psum_val", bufs=4))
+
+        ident_f32 = const.tile([P, P], F32)
+        make_identity(nc, ident_f32[:])
+        ident_bf16 = const.tile([P, P], BF16)
+        make_identity(nc, ident_bf16[:])
+
+        warm = const.tile([P, 1], F32)
+        nc.vector.memset(warm[:], 0.0)
+        nc.scalar.activation(out=warm[:], in_=warm[:], func=ACT.Exp)
+
+        qs_sb = const.tile([P, PIX], BF16)
+        nc.sync.dma_start(out=qs_sb[:], in_=qs_dram)
+        qe_sb = const.tile([P, PIX], BF16)
+        nc.sync.dma_start(out=qe_sb[:], in_=qe_dram)
+        qk_sb = const.tile([P, PIX], BF16)
+        nc.sync.dma_start(out=qk_sb[:], in_=qk_dram)
+
+        qs_twice = const.tile([P, PIX], BF16)
+        nc.vector.tensor_scalar(
+            out=qs_twice[:], in0=qs_sb[:], scalar1=2.0, scalar2=None, op0=ALU.mult
+        )
+        qe_minus = const.tile([P, PIX], BF16)
+        nc.vector.tensor_scalar(
+            out=qe_minus[:], in0=qe_sb[:], scalar1=-1.0, scalar2=None, op0=ALU.mult
+        )
+
+        def load_values(g):
+            raw = raw_pool.tile([P, VAL_TILES, K_PASS], BF16)
+            nc.sync.dma_start(out=raw[:], in_=mv_dram[:, :, g * K_PASS : (g + 1) * K_PASS])
+            return raw
+
+        def transpose_values(raw):
+            banks = []
+            for h in range(VAL // HALF_VAL):
+                bank = psum_val.tile([P, 2, HALF_VAL], F32)
+                for u in range(2):
+                    for q in range(HALF_VAL // P):
+                        words = raw[:, h * (HALF_VAL // P) + q, :].bitcast(F32)
+                        nc.tensor.transpose(
+                            bank[:, u, q * P : (q + 1) * P],
+                            words[:, u : 2 * P : 2],
+                            ident_f32[:],
+                        )
+                banks.append(bank)
+            return banks
+
+        def copy_values(banks, grouped):
+            pairs = grouped[:].rearrange("i (v u) -> i v u", u=2)
+            for h in range(VAL // HALF_VAL):
+                nc.scalar.copy(
+                    out=pairs[:, h * HALF_VAL : (h + 1) * HALF_VAL, :],
+                    in_=banks[h][:].rearrange("i u v -> i v u"),
+                )
+
+        w = [
+            [sim_pool.tile([P, CHUNK], F32, name="w%d_%d" % (pt, j)) for j in range(CHUNKS)]
+            for pt in range(PIX_TILES)
+        ]
+        chunk_max = const.tile([P, PIX_TILES, CHUNKS], F32)
+        e_sums = const.tile([P, PIX_TILES, PASSES], F32)
+        nc.vector.memset(e_sums[:], 0.0)
+        early = [
+            early_pool.tile([P, 2 * VAL], F32, name="early%d" % j, align_bytes=64)
+            for j in range(CHUNKS)
+        ]
+
+        with ExitStack() as phase:
+            stream = phase.enter_context(tc.tile_pool(name="stream", bufs=2))
+            psum_sim = phase.enter_context(tc.psum_pool(name="psum_sim", bufs=4))
+
+            qk_sq = const.tile([P, PIX], F32)
+            nc.vector.tensor_tensor(out=qk_sq[:], in0=qk_sb[:], in1=qk_sb[:], op=ALU.mult)
+            b_terms = const.tile([P, PIX], F32)
+            nc.vector.tensor_tensor(out=b_terms[:], in0=qk_sq[:], in1=qe_sb[:], op=ALU.mult)
+            b_bank = psum_sim.tile([P, PIX_TILES, P], F32, tag="u")
+            for pt in range(PIX_TILES):
+                nc.tensor.transpose(
+                    b_bank[:, pt, :], b_terms[:, pt * P : (pt + 1) * P], ident_f32[:]
+                )
+            b_sq = const.tile([P, PIX_TILES], F32)
+            nc.vector.reduce_sum(out=b_sq[:], in_=b_bank[:], axis=AXIS.X)
+            b_minus = const.tile([P, PIX_TILES], F32)
+            nc.vector.tensor_scalar(
+                out=b_minus[:], in0=b_sq[:], scalar1=-1.0, scalar2=None, op0=ALU.mult
+            )
+
+            for j in range(CHUNKS):
+                slots = slice(j * CHUNK, (j + 1) * CHUNK)
+                mk_sb = stream.tile([P, CHUNK], BF16)
+                nc.sync.dma_start(out=mk_sb[:], in_=mk_dram[:, slots])
+                m2_sb = stream.tile([P, CHUNK], BF16)
+                nc.sync.dma_start(out=m2_sb[:], in_=m2_dram[:, slots])
+                ms_sb = stream.tile([P, CHUNK], BF16)
+                nc.sync.dma_start(out=ms_sb[:], in_=ms_dram[slots].partition_broadcast(P))
+                raw = load_values(j * PASSES_PER_CHUNK)
+
+                for s in range(PASSES_PER_CHUNK):
+                    cols = slice(s * K_PASS, (s + 1) * K_PASS)
+                    mk_cols = mk_sb[:, cols].rearrange("c (m e) -> c e m", e=2)
+                    m2_cols = m2_sb[:, cols].rearrange("c (m e) -> c e m", e=2)
+                    ms_cols = ms_sb[:, cols].rearrange("c (m e) -> c e m", e=2)
+                    for pt in range(PIX_TILES):
+                        pixels = slice(pt * P, (pt + 1) * P)
+                        u = psum_sim.tile([P, 2, K_PASS // 2], F32, tag="u")
+                        nc.tensor.matmul(
+                            u[:], lhsT=qs_twice[:, pixels], rhs=mk_cols, start=True, stop=False
+                        )
+                        nc.tensor.matmul(
+                            u[:], lhsT=qe_minus[:, pixels], rhs=m2_cols, start=False, stop=True
+                        )
+                        w_cols = w[pt][j][:, cols].rearrange("p (e m) -> p e m", e=2)
+                        if pt == 0:
+                            nc.vector.scalar_tensor_tensor(
+                                out=w_cols,
+                                in0=u[:],
+                                scalar=b_sq[:, pt : pt + 1],
+                                in1=ms_cols,
+                                op0=ALU.subtract,
+                                op1=ALU.mult,
+                            )
+                        else:
+                            nc.scalar.activation(
+                                out=w_cols, in_=u[:], func=ACT.Identity, bias=b_minus[:, pt : pt + 1]
+                            )
+                            nc.gpsimd.tensor_tensor(
+                                out=w_cols, in0=w_cols, in1=ms_cols, op=ALU.mult
+                            )
+                copy_values(transpose_values(raw), early[j])
+                nc.vector.reduce_max(out=chunk_max[:, 0, j : j + 1], in_=w[0][j][:], axis=AXIS.X)
+                if j > 0:
+                    nc.vector.reduce_max(
+                        out=chunk_max[:, 1, j - 1 : j], in_=w[1][j - 1][:], axis=AXIS.X
+                    )
+            nc.vector.reduce_max(
+                out=chunk_max[:, 1, CHUNKS - 1 : CHUNKS], in_=w[1][CHUNKS - 1][:], axis=AXIS.X
+            )
+
+        w_max = const.tile([P, PIX_TILES], F32)
+        nc.vector.reduce_max(out=w_max[:], in_=chunk_max[:], axis=AXIS.X)
+        shift = const.tile([P, PIX_TILES], F32)
+        nc.vector.tensor_scalar(
+            out=shift[:], in0=w_max[:], scalar1=-INV_SQRT_CK, scalar2=None, op0=ALU.mult
+        )
+
+        psum_acc = whole.enter_context(tc.psum_pool(name="psum_acc", bufs=1))
+        acc = [psum_acc.tile([P, VAL], F32, name="acc%d" % pt) for pt in range(PIX_TILES)]
+
+        with ExitStack() as phase:
+            phase.enter_context(tc.manual_schedule())
+            e_pool = phase.enter_context(tc.tile_pool(name="e", bufs=3))
+            mx_pool = phase.enter_context(tc.tile_pool(name="mx", bufs=3))
+            psum_e = phase.enter_context(tc.psum_pool(name="psum_e", bufs=2))
+
+            e_sb = {}
+            e_banks = {}
+            mv_banks = {}
+            e_grouped = {}
+            mv_grouped = {}
+            codes = {}
+
+            def exponential(pt, q, first, count):
+                if first == 0:
+                    e_sb[(pt, q)] = e_pool.tile([P, PAIR], BF16, name="e%d" % pt, tag="e%d" % pt)
+                j, half = divmod(q, PAIRS_PER_CHUNK)
+                cols = slice(first * K_PASS, (first + count) * K_PASS)
+                w_cols = slice(half * PAIR + first * K_PASS, half * PAIR + (first + count) * K_PASS)
+                g = 2 * q + first
+                nc.scalar.activation(
+                    out=e_sb[(pt, q)][:, cols],
+                    in_=w[pt][j][:, w_cols],
+                    func=ACT.Exp,
+                    bias=shift[:, pt : pt + 1],
+                    scale=INV_SQRT_CK,
+                    accum_out=e_sums[:, pt, g : g + 1],
+                )
+
+            def transposes(g):
+                q, s = divmod(g, 2)
+                bank = psum_e.tile([P, 4, PIX], BF16)
+                for pt in range(PIX_TILES):
+                    for e in range(2):
+                        for u in range(2):
+                            first = s * K_PASS + e * (K_PASS // 2)
+                            nc.tensor.transpose(
+                                bank[:, 2 * u + e, pt * P : (pt + 1) * P],
+                                e_sb[(pt, q)][:, first + u : first + 2 * P : 2],
+                                ident_bf16[:],
+                            )
+                e_banks[g] = bank
+                if g % PASSES_PER_CHUNK != 0:
+                    mv_banks[g] = transpose_values(load_values(g))
+
+            def copies(g):
+                e_four = grouped_pool.tile([P, PIX, 4], BF16, align_bytes=64)
+                nc.vector.tensor_copy(
+                    out=e_four[:], in_=e_banks[g][:].rearrange("i t p -> i p t")
+                )
+                e_grouped[g] = e_four
+                if g % PASSES_PER_CHUNK == 0:
+                    mv_grouped[g] = early[g // PASSES_PER_CHUNK]
+                else:
+                    mv_four = grouped_pool.tile([P, 2 * VAL], F32, align_bytes=64)
+                    copy_values(mv_banks[g], mv_four)
+                    mv_grouped[g] = mv_four
+
+            def quantise(g):
+                e_codes = mx_pool.tile([P, PIX], U32, align_bytes=64)
+                e_scales = mx_pool.tile([P, PIX], U8, align_bytes=64)
+                nc.vector.quantize_mx(
+                    out=e_codes[:].bitcast(FP8X4),
+                    scales=e_scales[:],
+                    in_=e_grouped[g][:].rearrange("i p t -> i (p t)"),
+                )
+                mv_codes = mx_pool.tile([P, VAL], U32, align_bytes=64)
+                mv_scales = mx_pool.tile([P, VAL], U8, align_bytes=64)
+                nc.vector.quantize_mx(
+                    out=mv_codes[:].bitcast(FP8X4),
+                    scales=mv_scales[:],
+                    in_=mv_grouped[g][:].bitcast(BF16),
+                )
+                codes[g] = (e_codes, e_scales, mv_codes, mv_scales)
+
+            def readout(g):
+                e_codes, e_scales, mv_codes, mv_scales = codes[g]
+                for pt in range(PIX_TILES):
+                    pixels = slice(pt * P, (pt + 1) * P)
+                    nc.tensor.matmul_mx(
+                        out=acc[pt][:],
+                        lhsT=e_codes[:, pixels].bitcast(FP8X4),
+                        lhsT_scale=e_scales[:, pixels],
+                        rhs=mv_codes[:].bitcast(FP8X4),
+                        rhs_scale=mv_scales[:],
+                        start=(g == 0),
+                        stop=(g == PASSES - 1),
+                    )
+
+            for first in range(2):
+                for pt in range(PIX_TILES):
+                    exponential(pt, 0, first, 1)
+            exponential(0, 1, 0, 2)
+            for k in range(PASSES + 3):
+                if k < PASSES:
+                    transposes(k)
+                if 1 <= k <= PASSES:
+                    copies(k - 1)
+                if (k + 3) // 2 < PAIRS:
+                    exponential((k + 1) % 2, (k + 3) // 2, 0, 2)
+                if 2 <= k <= PASSES + 1:
+                    quantise(k - 2)
+                if k >= 3:
+                    readout(k - 3)
+
+        with tc.tile_pool(name="tail", bufs=2) as tail:
+            total = const.tile([P, PIX_TILES], F32)
+            nc.vector.reduce_sum(out=total[:], in_=e_sums[:], axis=AXIS.X)
+            inv_total = const.tile([P, PIX_TILES], F32)
+            nc.vector.reciprocal(out=inv_total[:], in_=total[:])
+
+            mem0 = tail.tile([P, VAL], F32)
+            nc.vector.tensor_scalar(
+                out=mem0[:], in0=acc[0][:], scalar1=inv_total[:, 0:1], scalar2=None, op0=ALU.mult
+            )
+            mem1 = tail.tile([P, VAL], F32)
+            nc.scalar.activation(
+                out=mem1[:], in_=acc[1][:], func=ACT.Copy, scale=inv_total[:, 1:2]
+            )
+            mem = [mem0, mem1]
+            for h in range(VAL // HALF_VAL):
+                bank = psum_val.tile([P, 2, PIX], F32)
+                for q in range(2):
+                    channels = slice((2 * h + q) * P, (2 * h + q + 1) * P)
+                    for pt in range(PIX_TILES):
+                        nc.tensor.transpose(
+                            bank[:, q, pt * P : (pt + 1) * P], mem[pt][:, channels], ident_f32[:]
+                        )
+                result = tail.tile([P, 2, PIX], F32)
+                if h == 0:
+                    nc.vector.tensor_copy(out=result[:], in_=bank[:])
+                else:
+                    nc.scalar.copy(out=result[:], in_=bank[:])
+                nc.sync.dma_start(out=out_dram[:, 2 * h : 2 * h + 2, :], in_=result[:])

@@ -23,13 +23,14 @@ VAL_TILES = VAL // P
 HALF_VAL = VAL // 2
 K_PASS = 4 * P
 PASSES = SLOTS // K_PASS
-CHUNK = 2048
-CHUNKS = SLOTS // CHUNK
-PASSES_PER_CHUNK = CHUNK // K_PASS
 PAIR = 2 * K_PASS
 PAIRS = SLOTS // PAIR
-PAIRS_PER_CHUNK = CHUNK // PAIR
-INV_SQRT_CK = 1.0 / math.sqrt(CK)
+EXP_SCALE = 2.0 / math.sqrt(CK)
+
+EARLY_COUNT = 9
+EARLY = [4 + (i * (PASSES - 4)) // EARLY_COUNT for i in range(EARLY_COUNT)]
+EARLY_STEP = [3 + (i * (PASSES - 5)) // EARLY_COUNT for i in range(EARLY_COUNT)]
+LATE = [g for g in range(PASSES) if g not in EARLY]
 
 FLOPS = 2 * SLOTS * PIX * (2 * CK + VAL)
 
@@ -59,262 +60,329 @@ def tile_xmem_pa_k_kernel(
     out_dram = out.rearrange("b o c h w -> (b o c) (h w)").rearrange("(q r) p -> r q p", r=P)
 
     with ExitStack() as whole:
+        whole.enter_context(tc.manual_schedule())
         const = whole.enter_context(tc.tile_pool(name="const", bufs=1))
         sim_pool = whole.enter_context(tc.tile_pool(name="sim", bufs=1))
         early_pool = whole.enter_context(tc.tile_pool(name="early", bufs=1))
         raw_pool = whole.enter_context(tc.tile_pool(name="raw", bufs=4))
-        grouped_pool = whole.enter_context(tc.tile_pool(name="grouped", bufs=3))
+        grouped_pool = whole.enter_context(tc.tile_pool(name="grouped", bufs=4))
+        e_grouped_pool = whole.enter_context(tc.tile_pool(name="e_grouped", bufs=3))
         psum_val = whole.enter_context(tc.psum_pool(name="psum_val", bufs=4))
 
-        ident_f32 = const.tile([P, P], F32)
-        make_identity(nc, ident_f32[:])
-        ident_bf16 = const.tile([P, P], BF16)
-        make_identity(nc, ident_bf16[:])
-
-        warm = const.tile([P, 1], F32)
-        nc.vector.memset(warm[:], 0.0)
-        nc.scalar.activation(out=warm[:], in_=warm[:], func=ACT.Exp)
-
-        qs_sb = const.tile([P, PIX], BF16)
-        nc.sync.dma_start(out=qs_sb[:], in_=qs_dram)
-        qe_sb = const.tile([P, PIX], BF16)
-        nc.sync.dma_start(out=qe_sb[:], in_=qe_dram)
-        qk_sb = const.tile([P, PIX], BF16)
-        nc.sync.dma_start(out=qk_sb[:], in_=qk_dram)
-
-        qs_twice = const.tile([P, PIX], BF16)
-        nc.vector.tensor_scalar(
-            out=qs_twice[:], in0=qs_sb[:], scalar1=2.0, scalar2=None, op0=ALU.mult
-        )
-        qe_minus = const.tile([P, PIX], BF16)
-        nc.vector.tensor_scalar(
-            out=qe_minus[:], in0=qe_sb[:], scalar1=-1.0, scalar2=None, op0=ALU.mult
-        )
+        raws = {}
+        mv_banks = {}
+        mv_grouped = {}
 
         def load_values(g):
             raw = raw_pool.tile([P, VAL_TILES, K_PASS], BF16)
             nc.sync.dma_start(out=raw[:], in_=mv_dram[:, :, g * K_PASS : (g + 1) * K_PASS])
-            return raw
+            raws[g] = raw
 
-        def transpose_values(raw):
+        def transpose_values(g):
             banks = []
             for h in range(VAL // HALF_VAL):
                 bank = psum_val.tile([P, 2, HALF_VAL], F32)
                 for u in range(2):
                     for q in range(HALF_VAL // P):
-                        words = raw[:, h * (HALF_VAL // P) + q, :].bitcast(F32)
+                        words = raws[g][:, h * (HALF_VAL // P) + q, :].bitcast(F32)
                         nc.tensor.transpose(
                             bank[:, u, q * P : (q + 1) * P],
                             words[:, u : 2 * P : 2],
                             ident_f32[:],
                         )
                 banks.append(bank)
-            return banks
+            mv_banks[g] = banks
 
-        def copy_values(banks, grouped):
-            pairs = grouped[:].rearrange("i (v u) -> i v u", u=2)
-            for h in range(VAL // HALF_VAL):
-                nc.scalar.copy(
-                    out=pairs[:, h * HALF_VAL : (h + 1) * HALF_VAL, :],
-                    in_=banks[h][:].rearrange("i u v -> i v u"),
-                )
+        def copy_values(g, h, copy):
+            pairs = mv_grouped[g][:].rearrange("i (v u) -> i v u", u=2)
+            copy(
+                out=pairs[:, h * HALF_VAL : (h + 1) * HALF_VAL, :],
+                in_=mv_banks[g][h][:].rearrange("i u v -> i v u"),
+            )
 
         w = [
-            [sim_pool.tile([P, CHUNK], F32, name="w%d_%d" % (pt, j)) for j in range(CHUNKS)]
+            [sim_pool.tile([P, PAIR], F32, name="w%d_%d" % (pt, q)) for q in range(PAIRS)]
             for pt in range(PIX_TILES)
         ]
-        chunk_max = const.tile([P, PIX_TILES, CHUNKS], F32)
-        e_sums = const.tile([P, PIX_TILES, PASSES], F32)
-        nc.vector.memset(e_sums[:], 0.0)
-        early = [
-            early_pool.tile([P, 2 * VAL], F32, name="early%d" % j, align_bytes=64)
-            for j in range(CHUNKS)
-        ]
+        for g in EARLY:
+            mv_grouped[g] = early_pool.tile([P, 2 * VAL], F32, name="early%d" % g, align_bytes=64)
 
-        with ExitStack() as phase:
-            stream = phase.enter_context(tc.tile_pool(name="stream", bufs=2))
-            psum_sim = phase.enter_context(tc.psum_pool(name="psum_sim", bufs=4))
+        with ExitStack() as phase1:
+            stream = phase1.enter_context(tc.tile_pool(name="stream", bufs=3))
+            psum_sim = phase1.enter_context(tc.psum_pool(name="psum_sim", bufs=4))
 
+            keys = {}
+
+            def load_keys(q):
+                slots = slice(q * PAIR, (q + 1) * PAIR)
+                mk_sb = stream.tile([P, PAIR], BF16)
+                nc.sync.dma_start(out=mk_sb[:], in_=mk_dram[:, slots])
+                m2_sb = stream.tile([P, PAIR], BF16)
+                nc.sync.dma_start(out=m2_sb[:], in_=m2_dram[:, slots])
+                ms_sb = stream.tile([P, PAIR], BF16)
+                nc.sync.dma_start(out=ms_sb[:], in_=ms_dram[slots].partition_broadcast(P))
+                keys[q] = (mk_sb, m2_sb, ms_sb)
+
+            qs_sb = const.tile([P, PIX], BF16)
+            nc.sync.dma_start(out=qs_sb[:], in_=qs_dram)
+            qe_sb = const.tile([P, PIX], BF16)
+            nc.sync.dma_start(out=qe_sb[:], in_=qe_dram)
+            qk_sb = const.tile([P, PIX], BF16)
+            nc.sync.dma_start(out=qk_sb[:], in_=qk_dram)
+            load_keys(0)
+            load_keys(1)
+
+            warm = const.tile([P, 1], F32)
+            nc.vector.memset(warm[:], 0.0)
+            nc.scalar.activation(out=warm[:], in_=warm[:], func=ACT.Exp)
+            ident_f32 = const.tile([P, P], F32)
+            make_identity(nc, ident_f32[:])
+
+            qe_half = const.tile([P, PIX], BF16)
+            nc.vector.tensor_scalar(
+                out=qe_half[:], in0=qe_sb[:], scalar1=-0.5, scalar2=None, op0=ALU.mult
+            )
             qk_sq = const.tile([P, PIX], F32)
             nc.vector.tensor_tensor(out=qk_sq[:], in0=qk_sb[:], in1=qk_sb[:], op=ALU.mult)
             b_terms = const.tile([P, PIX], F32)
             nc.vector.tensor_tensor(out=b_terms[:], in0=qk_sq[:], in1=qe_sb[:], op=ALU.mult)
-            b_bank = psum_sim.tile([P, PIX_TILES, P], F32, tag="u")
-            for pt in range(PIX_TILES):
-                nc.tensor.transpose(
-                    b_bank[:, pt, :], b_terms[:, pt * P : (pt + 1) * P], ident_f32[:]
-                )
-            b_sq = const.tile([P, PIX_TILES], F32)
-            nc.vector.reduce_sum(out=b_sq[:], in_=b_bank[:], axis=AXIS.X)
+            b_sum = const.tile([P, PIX_TILES], F32)
             b_minus = const.tile([P, PIX_TILES], F32)
-            nc.vector.tensor_scalar(
-                out=b_minus[:], in0=b_sq[:], scalar1=-1.0, scalar2=None, op0=ALU.mult
-            )
 
-            for j in range(CHUNKS):
-                slots = slice(j * CHUNK, (j + 1) * CHUNK)
-                mk_sb = stream.tile([P, CHUNK], BF16)
-                nc.sync.dma_start(out=mk_sb[:], in_=mk_dram[:, slots])
-                m2_sb = stream.tile([P, CHUNK], BF16)
-                nc.sync.dma_start(out=m2_sb[:], in_=m2_dram[:, slots])
-                ms_sb = stream.tile([P, CHUNK], BF16)
-                nc.sync.dma_start(out=ms_sb[:], in_=ms_dram[slots].partition_broadcast(P))
-                raw = load_values(j * PASSES_PER_CHUNK)
-
-                for s in range(PASSES_PER_CHUNK):
-                    cols = slice(s * K_PASS, (s + 1) * K_PASS)
-                    mk_cols = mk_sb[:, cols].rearrange("c (m e) -> c e m", e=2)
-                    m2_cols = m2_sb[:, cols].rearrange("c (m e) -> c e m", e=2)
-                    ms_cols = ms_sb[:, cols].rearrange("c (m e) -> c e m", e=2)
-                    for pt in range(PIX_TILES):
-                        pixels = slice(pt * P, (pt + 1) * P)
-                        u = psum_sim.tile([P, 2, K_PASS // 2], F32, tag="u")
-                        nc.tensor.matmul(
-                            u[:], lhsT=qs_twice[:, pixels], rhs=mk_cols, start=True, stop=False
-                        )
-                        nc.tensor.matmul(
-                            u[:], lhsT=qe_minus[:, pixels], rhs=m2_cols, start=False, stop=True
-                        )
-                        w_cols = w[pt][j][:, cols].rearrange("p (e m) -> p e m", e=2)
-                        if pt == 0:
-                            nc.vector.scalar_tensor_tensor(
-                                out=w_cols,
-                                in0=u[:],
-                                scalar=b_sq[:, pt : pt + 1],
-                                in1=ms_cols,
-                                op0=ALU.subtract,
-                                op1=ALU.mult,
-                            )
-                        else:
-                            nc.scalar.activation(
-                                out=w_cols, in_=u[:], func=ACT.Identity, bias=b_minus[:, pt : pt + 1]
-                            )
-                            nc.gpsimd.tensor_tensor(
-                                out=w_cols, in0=w_cols, in1=ms_cols, op=ALU.mult
-                            )
-                copy_values(transpose_values(raw), early[j])
-                nc.vector.reduce_max(out=chunk_max[:, 0, j : j + 1], in_=w[0][j][:], axis=AXIS.X)
-                if j > 0:
-                    nc.vector.reduce_max(
-                        out=chunk_max[:, 1, j - 1 : j], in_=w[1][j - 1][:], axis=AXIS.X
+            def sum_b():
+                b_bank = psum_sim.tile([P, PIX_TILES, P], F32, tag="u")
+                for pt in range(PIX_TILES):
+                    nc.tensor.transpose(
+                        b_bank[:, pt, :], b_terms[:, pt * P : (pt + 1) * P], ident_f32[:]
                     )
-            nc.vector.reduce_max(
-                out=chunk_max[:, 1, CHUNKS - 1 : CHUNKS], in_=w[1][CHUNKS - 1][:], axis=AXIS.X
-            )
+                nc.vector.reduce_sum(out=b_sum[:], in_=b_bank[:], axis=AXIS.X)
+                nc.vector.tensor_scalar(
+                    out=b_minus[:], in0=b_sum[:], scalar1=-0.5, scalar2=None, op0=ALU.mult
+                )
 
-        w_max = const.tile([P, PIX_TILES], F32)
-        nc.vector.reduce_max(out=w_max[:], in_=chunk_max[:], axis=AXIS.X)
-        shift = const.tile([P, PIX_TILES], F32)
-        nc.vector.tensor_scalar(
-            out=shift[:], in0=w_max[:], scalar1=-INV_SQRT_CK, scalar2=None, op0=ALU.mult
-        )
+            u_banks = {}
+            pair_max = const.tile([P, PIX_TILES, PAIRS], F32)
+            w_max = const.tile([P, PIX_TILES], F32)
+            shift = const.tile([P, PIX_TILES], F32)
+
+            def by_word(ap):
+                return ap.rearrange("p (i u e) -> p u i e", u=2, e=2)
+
+            def pass_columns(s):
+                return slice((s % 2) * K_PASS, (s % 2 + 1) * K_PASS)
+
+            def similarities(s):
+                mk_sb, m2_sb, ms_sb = keys[s // 2]
+                cols = pass_columns(s)
+                for pt in range(PIX_TILES):
+                    pixels = slice(pt * P, (pt + 1) * P)
+                    u = psum_sim.tile([P, K_PASS], F32, tag="u")
+                    nc.tensor.matmul(
+                        u[:],
+                        lhsT=qs_sb[:, pixels],
+                        rhs=by_word(mk_sb[:, cols]),
+                        start=True,
+                        stop=False,
+                    )
+                    nc.tensor.matmul(
+                        u[:],
+                        lhsT=qe_half[:, pixels],
+                        rhs=by_word(m2_sb[:, cols]),
+                        start=False,
+                        stop=True,
+                    )
+                    u_banks[(pt, s)] = u
+
+            def empty_on_vector(pt, s):
+                ms_cols = by_word(keys[s // 2][2][:, pass_columns(s)])
+                w_cols = w[pt][s // 2][:, pass_columns(s)].rearrange("p (u i e) -> p u i e", u=2, e=2)
+                u = u_banks[(pt, s)][:].rearrange("p (u i e) -> p u i e", u=2, e=2)
+                for half in range(2):
+                    nc.vector.scalar_tensor_tensor(
+                        out=w_cols[:, half],
+                        in0=u[:, half],
+                        scalar=b_minus[:, pt : pt + 1],
+                        in1=ms_cols[:, half],
+                        op0=ALU.add,
+                        op1=ALU.mult,
+                    )
+
+            def empty_on_scalar(pt, s):
+                w_cols = w[pt][s // 2][:, pass_columns(s)]
+                nc.scalar.activation(
+                    out=w_cols,
+                    in_=u_banks[(pt, s)][:],
+                    func=ACT.Identity,
+                    bias=b_minus[:, pt : pt + 1],
+                )
+                w_words = w_cols.rearrange("p (u i e) -> p u i e", u=2, e=2)
+                nc.gpsimd.tensor_tensor(
+                    out=w_words,
+                    in0=w_words,
+                    in1=by_word(keys[s // 2][2][:, pass_columns(s)]),
+                    op=ALU.mult,
+                )
+
+            def maximum(pt, q):
+                nc.vector.reduce_max(
+                    out=pair_max[:, pt, q : q + 1], in_=w[pt][q][:], axis=AXIS.X
+                )
+
+            def find_shift(pt):
+                nc.vector.reduce_max(
+                    out=w_max[:, pt : pt + 1], in_=pair_max[:, pt, :], axis=AXIS.X
+                )
+                nc.vector.tensor_scalar(
+                    out=shift[:, pt : pt + 1],
+                    in0=w_max[:, pt : pt + 1],
+                    scalar1=-EXP_SCALE,
+                    scalar2=None,
+                    op0=ALU.mult,
+                )
+
+            to_copy = []
+            for s in range(PASSES):
+                if s % 2 == 0 and s // 2 + 2 < PAIRS:
+                    load_keys(s // 2 + 2)
+                for g, step in zip(EARLY, EARLY_STEP):
+                    if s == max(0, step - 3):
+                        load_values(g)
+                if s == PASSES - 4:
+                    load_values(0)
+                if s == PASSES - 2:
+                    load_values(1)
+                similarities(s)
+                if s == 0:
+                    sum_b()
+                for g in to_copy:
+                    copy_values(g, 0, nc.scalar.copy)
+                empty_on_vector(0, s)
+                if s >= PASSES - 2:
+                    empty_on_vector(1, s)
+                else:
+                    empty_on_scalar(1, s)
+                for g in to_copy:
+                    copy_values(g, 1, nc.scalar.copy)
+                to_copy = []
+                for g, step in zip(EARLY, EARLY_STEP):
+                    if s == step:
+                        transpose_values(g)
+                        to_copy.append(g)
+                if s % 2 == 0 and s >= 2:
+                    maximum(0, s // 2 - 1)
+                if s % 2 == 1 and s >= 3:
+                    maximum(1, (s - 3) // 2)
+            for g in to_copy:
+                copy_values(g, 0, nc.scalar.copy)
+                copy_values(g, 1, nc.scalar.copy)
+            for pt in range(PIX_TILES):
+                maximum(pt, PAIRS - 1)
+                find_shift(pt)
 
         psum_acc = whole.enter_context(tc.psum_pool(name="psum_acc", bufs=1))
         acc = [psum_acc.tile([P, VAL], F32, name="acc%d" % pt) for pt in range(PIX_TILES)]
+        e_sums = const.tile([P, PIX_TILES, PAIRS + 1], F32)
 
         with ExitStack() as phase:
-            phase.enter_context(tc.manual_schedule())
             e_pool = phase.enter_context(tc.tile_pool(name="e", bufs=3))
-            mx_pool = phase.enter_context(tc.tile_pool(name="mx", bufs=3))
+            e_mx_pool = phase.enter_context(tc.tile_pool(name="e_mx", bufs=3))
+            mv_mx_pool = phase.enter_context(tc.tile_pool(name="mv_mx", bufs=4))
             psum_e = phase.enter_context(tc.psum_pool(name="psum_e", bufs=2))
 
             e_sb = {}
             e_banks = {}
-            mv_banks = {}
             e_grouped = {}
-            mv_grouped = {}
-            codes = {}
+            e_codes = {}
+            mv_codes = {}
 
-            def exponential(pt, q, first, count):
-                if first == 0:
+            def exponential(pt, q, cols, column):
+                if (pt, q) not in e_sb:
                     e_sb[(pt, q)] = e_pool.tile([P, PAIR], BF16, name="e%d" % pt, tag="e%d" % pt)
-                j, half = divmod(q, PAIRS_PER_CHUNK)
-                cols = slice(first * K_PASS, (first + count) * K_PASS)
-                w_cols = slice(half * PAIR + first * K_PASS, half * PAIR + (first + count) * K_PASS)
-                g = 2 * q + first
                 nc.scalar.activation(
                     out=e_sb[(pt, q)][:, cols],
-                    in_=w[pt][j][:, w_cols],
+                    in_=w[pt][q][:, cols],
                     func=ACT.Exp,
                     bias=shift[:, pt : pt + 1],
-                    scale=INV_SQRT_CK,
-                    accum_out=e_sums[:, pt, g : g + 1],
+                    scale=EXP_SCALE,
+                    accum_out=e_sums[:, pt, column : column + 1],
                 )
 
-            def transposes(g):
+            def transpose_e(g):
                 q, s = divmod(g, 2)
-                bank = psum_e.tile([P, 4, PIX], BF16)
+                bank = psum_e.tile([P, 2, PIX], F32)
                 for pt in range(PIX_TILES):
-                    for e in range(2):
-                        for u in range(2):
-                            first = s * K_PASS + e * (K_PASS // 2)
-                            nc.tensor.transpose(
-                                bank[:, 2 * u + e, pt * P : (pt + 1) * P],
-                                e_sb[(pt, q)][:, first + u : first + 2 * P : 2],
-                                ident_bf16[:],
-                            )
+                    words = e_sb[(pt, q)][:].bitcast(F32)
+                    for u in range(2):
+                        first = s * (K_PASS // 2) + u * P
+                        nc.tensor.transpose(
+                            bank[:, u, pt * P : (pt + 1) * P],
+                            words[:, first : first + P],
+                            ident_f32[:],
+                        )
                 e_banks[g] = bank
-                if g % PASSES_PER_CHUNK != 0:
-                    mv_banks[g] = transpose_values(load_values(g))
 
-            def copies(g):
-                e_four = grouped_pool.tile([P, PIX, 4], BF16, align_bytes=64)
+            def copy_e(g):
+                e_four = e_grouped_pool.tile([P, PIX, 2], F32, align_bytes=64)
                 nc.vector.tensor_copy(
-                    out=e_four[:], in_=e_banks[g][:].rearrange("i t p -> i p t")
+                    out=e_four[:], in_=e_banks[g][:].rearrange("i u p -> i p u")
                 )
                 e_grouped[g] = e_four
-                if g % PASSES_PER_CHUNK == 0:
-                    mv_grouped[g] = early[g // PASSES_PER_CHUNK]
-                else:
-                    mv_four = grouped_pool.tile([P, 2 * VAL], F32, align_bytes=64)
-                    copy_values(mv_banks[g], mv_four)
-                    mv_grouped[g] = mv_four
 
-            def quantise(g):
-                e_codes = mx_pool.tile([P, PIX], U32, align_bytes=64)
-                e_scales = mx_pool.tile([P, PIX], U8, align_bytes=64)
+            def quantise(words, columns, pool):
+                codes = pool.tile([P, columns], U32, align_bytes=64)
+                scales = pool.tile([P, columns], U8, align_bytes=64)
                 nc.vector.quantize_mx(
-                    out=e_codes[:].bitcast(FP8X4),
-                    scales=e_scales[:],
-                    in_=e_grouped[g][:].rearrange("i p t -> i (p t)"),
+                    out=codes[:].bitcast(FP8X4), scales=scales[:], in_=words.bitcast(BF16)
                 )
-                mv_codes = mx_pool.tile([P, VAL], U32, align_bytes=64)
-                mv_scales = mx_pool.tile([P, VAL], U8, align_bytes=64)
-                nc.vector.quantize_mx(
-                    out=mv_codes[:].bitcast(FP8X4),
-                    scales=mv_scales[:],
-                    in_=mv_grouped[g][:].bitcast(BF16),
-                )
-                codes[g] = (e_codes, e_scales, mv_codes, mv_scales)
+                return codes, scales
 
             def readout(g):
-                e_codes, e_scales, mv_codes, mv_scales = codes[g]
                 for pt in range(PIX_TILES):
                     pixels = slice(pt * P, (pt + 1) * P)
                     nc.tensor.matmul_mx(
                         out=acc[pt][:],
-                        lhsT=e_codes[:, pixels].bitcast(FP8X4),
-                        lhsT_scale=e_scales[:, pixels],
-                        rhs=mv_codes[:].bitcast(FP8X4),
-                        rhs_scale=mv_scales[:],
+                        lhsT=e_codes[g][0][:, pixels].bitcast(FP8X4),
+                        lhsT_scale=e_codes[g][1][:, pixels],
+                        rhs=mv_codes[g][0][:].bitcast(FP8X4),
+                        rhs_scale=mv_codes[g][1][:],
                         start=(g == 0),
                         stop=(g == PASSES - 1),
                     )
 
-            for first in range(2):
-                for pt in range(PIX_TILES):
-                    exponential(pt, 0, first, 1)
-            exponential(0, 1, 0, 2)
-            for k in range(PASSES + 3):
-                if k < PASSES:
-                    transposes(k)
+            loads = LATE[2:]
+            for k in range(-2, PASSES + 4):
+                if k >= -2 and loads and k + 5 >= loads[0]:
+                    load_values(loads.pop(0))
+                if 0 <= k < PASSES:
+                    transpose_e(k)
+                if k + 2 in LATE:
+                    transpose_values(k + 2)
+                if k + 1 in LATE:
+                    mv_grouped[k + 1] = grouped_pool.tile([P, 2 * VAL], F32, align_bytes=64, name="mv_four")
+                    share = LATE.index(k + 1) % 2 == 1
+                    copy_values(k + 1, 0, nc.scalar.copy)
+                    if not share:
+                        copy_values(k + 1, 1, nc.scalar.copy)
+                if k == -1:
+                    first, second = slice(0, K_PASS), slice(K_PASS, PAIR)
+                    for pt in range(PIX_TILES):
+                        exponential(pt, 0, first, 0)
+                        exponential(pt, 0, second, PAIRS)
+                    exponential(0, 1, slice(0, PAIR), 1)
+                if k >= 0 and (k + 3) // 2 < PAIRS:
+                    exponential((k + 1) % 2, (k + 3) // 2, slice(0, PAIR), (k + 3) // 2)
                 if 1 <= k <= PASSES:
-                    copies(k - 1)
-                if (k + 3) // 2 < PAIRS:
-                    exponential((k + 1) % 2, (k + 3) // 2, 0, 2)
+                    copy_e(k - 1)
+                if k + 1 in LATE and share:
+                    copy_values(k + 1, 1, nc.vector.tensor_copy)
                 if 2 <= k <= PASSES + 1:
-                    quantise(k - 2)
-                if k >= 3:
+                    e_codes[k - 2] = quantise(
+                        e_grouped[k - 2][:].rearrange("i p u -> i (p u)"), PIX, e_mx_pool
+                    )
+                if 1 <= k <= PASSES:
+                    mv_codes[k - 1] = quantise(mv_grouped[k - 1][:], VAL, mv_mx_pool)
+                if k % 2 == 0 and 4 <= k <= PASSES + 2:
+                    readout(k - 4)
                     readout(k - 3)
 
         with tc.tile_pool(name="tail", bufs=2) as tail:

@@ -350,7 +350,7 @@ def tile_xmem_pa_k_kernel(
                     )
 
             loads = LATE[2:]
-            for k in range(-2, PASSES + 4):
+            for k in range(-2, PASSES + 3):
                 if k >= -2 and loads and k + 5 >= loads[0]:
                     load_values(loads.pop(0))
                 if 0 <= k < PASSES:
@@ -381,8 +381,7 @@ def tile_xmem_pa_k_kernel(
                     )
                 if 1 <= k <= PASSES:
                     mv_codes[k - 1] = quantise(mv_grouped[k - 1][:], VAL, mv_mx_pool)
-                if k % 2 == 0 and 4 <= k <= PASSES + 2:
-                    readout(k - 4)
+                if 3 <= k <= PASSES + 2:
                     readout(k - 3)
 
         with tc.tile_pool(name="tail", bufs=2) as tail:

@@ -25,6 +25,7 @@ K_PASS = 4 * P
 PASSES = SLOTS // K_PASS
 PAIR = 2 * K_PASS
 PAIRS = SLOTS // PAIR
+MS_ROWS = 2 * PASSES
 EXP_SCALE = 2.0 / math.sqrt(CK)
 
 EARLY_COUNT = 9
@@ -53,7 +54,9 @@ def tile_xmem_pa_k_kernel(
     qs_dram = qk_sel.rearrange("b c h w -> (b c) (h w)")
     mk_dram = memory_key.rearrange("b c t h w -> (b c) (t h w)")
     m2_dram = mk_sq.rearrange("b c t h w -> (b c) (t h w)")
-    ms_dram = memory_shrinkage.rearrange("b o t h w -> (b o t h w)")
+    ms_dram = memory_shrinkage.rearrange("b o t h w -> (b o t h w)").rearrange(
+        "(r n) -> r n", r=MS_ROWS
+    )
     mv_dram = memory_value.rearrange("b o c t h w -> (b o c) (t h w)").rearrange(
         "(q r) n -> r q n", r=P
     )
@@ -81,7 +84,7 @@ def tile_xmem_pa_k_kernel(
         def transpose_values(g):
             banks = []
             for h in range(VAL // HALF_VAL):
-                bank = psum_val.tile([P, 2, HALF_VAL], F32)
+                bank = psum_val.tile([P, 2, HALF_VAL], F32, tag="val")
                 for u in range(2):
                     for q in range(HALF_VAL // P):
                         words = raws[g][:, h * (HALF_VAL // P) + q, :].bitcast(F32)
@@ -119,10 +122,29 @@ def tile_xmem_pa_k_kernel(
                 nc.sync.dma_start(out=mk_sb[:], in_=mk_dram[:, slots])
                 m2_sb = stream.tile([P, PAIR], BF16)
                 nc.sync.dma_start(out=m2_sb[:], in_=m2_dram[:, slots])
-                ms_sb = stream.tile([P, PAIR], BF16)
-                nc.sync.dma_start(out=ms_sb[:], in_=ms_dram[slots].partition_broadcast(P))
-                keys[q] = (mk_sb, m2_sb, ms_sb)
+                keys[q] = (mk_sb, m2_sb)
 
+            ms_tiles = {}
+
+            def spread_shrinkage(q):
+                bank = psum_val.tile([P, PAIR], BF16, tag="val")
+                for s in (2 * q, 2 * q + 1):
+                    for u in range(2):
+                        for h in range(2):
+                            first = (s % 2) * K_PASS + u * 2 * P + h * P
+                            column = u * MS_ROWS + 2 * s + h
+                            nc.tensor.transpose(
+                                bank[:, first : first + P],
+                                ms_cols[:, column : column + 1].to_broadcast([P, P]),
+                                ident_bf16[:],
+                            )
+                ms_sb = stream.tile([P, PAIR], BF16)
+                nc.scalar.copy(out=ms_sb[:], in_=bank[:])
+                ms_tiles[q] = ms_sb
+
+            ms_rows = const.tile([P, 2 * P], BF16)
+            for u in range(2):
+                nc.sync.dma_start(out=ms_rows[u * MS_ROWS : (u + 1) * MS_ROWS, :], in_=ms_dram)
             qs_sb = const.tile([P, PIX], BF16)
             nc.sync.dma_start(out=qs_sb[:], in_=qs_dram)
             qe_sb = const.tile([P, PIX], BF16)
@@ -137,6 +159,20 @@ def tile_xmem_pa_k_kernel(
             nc.scalar.activation(out=warm[:], in_=warm[:], func=ACT.Exp)
             ident_f32 = const.tile([P, P], F32)
             make_identity(nc, ident_f32[:])
+            ident_bf16 = const.tile([P, P], BF16)
+            make_identity(nc, ident_bf16[:])
+
+            ms_pairs = const.tile([P, P], BF16)
+            for u in range(2):
+                rows = slice(u * MS_ROWS, (u + 1) * MS_ROWS)
+                nc.vector.tensor_copy(
+                    out=ms_pairs[rows, :].rearrange("r (i e) -> r i e", e=2),
+                    in_=ms_rows[rows, :].rearrange("r (i u e) -> r u i e", u=2, e=2)[:, u],
+                )
+            ms_bank = psum_val.tile([P, P], BF16, tag="val")
+            nc.tensor.transpose(ms_bank[:], ms_pairs[:], ident_bf16[:])
+            ms_cols = const.tile([P, P], BF16)
+            nc.vector.tensor_copy(out=ms_cols[:], in_=ms_bank[:])
 
             qe_half = const.tile([P, PIX], BF16)
             nc.vector.tensor_scalar(
@@ -172,7 +208,7 @@ def tile_xmem_pa_k_kernel(
                 return slice((s % 2) * K_PASS, (s % 2 + 1) * K_PASS)
 
             def similarities(s):
-                mk_sb, m2_sb, ms_sb = keys[s // 2]
+                mk_sb, m2_sb = keys[s // 2]
                 cols = pass_columns(s)
                 for pt in range(PIX_TILES):
                     pixels = slice(pt * P, (pt + 1) * P)
@@ -194,18 +230,14 @@ def tile_xmem_pa_k_kernel(
                     u_banks[(pt, s)] = u
 
             def empty_on_vector(pt, s):
-                ms_cols = by_word(keys[s // 2][2][:, pass_columns(s)])
-                w_cols = w[pt][s // 2][:, pass_columns(s)].rearrange("p (u i e) -> p u i e", u=2, e=2)
-                u = u_banks[(pt, s)][:].rearrange("p (u i e) -> p u i e", u=2, e=2)
-                for half in range(2):
-                    nc.vector.scalar_tensor_tensor(
-                        out=w_cols[:, half],
-                        in0=u[:, half],
-                        scalar=b_minus[:, pt : pt + 1],
-                        in1=ms_cols[:, half],
-                        op0=ALU.add,
-                        op1=ALU.mult,
-                    )
+                nc.vector.scalar_tensor_tensor(
+                    out=w[pt][s // 2][:, pass_columns(s)],
+                    in0=u_banks[(pt, s)][:],
+                    scalar=b_minus[:, pt : pt + 1],
+                    in1=ms_tiles[s // 2][:, pass_columns(s)],
+                    op0=ALU.add,
+                    op1=ALU.mult,
+                )
 
             def empty_on_scalar(pt, s):
                 w_cols = w[pt][s // 2][:, pass_columns(s)]
@@ -215,12 +247,8 @@ def tile_xmem_pa_k_kernel(
                     func=ACT.Identity,
                     bias=b_minus[:, pt : pt + 1],
                 )
-                w_words = w_cols.rearrange("p (u i e) -> p u i e", u=2, e=2)
                 nc.gpsimd.tensor_tensor(
-                    out=w_words,
-                    in0=w_words,
-                    in1=by_word(keys[s // 2][2][:, pass_columns(s)]),
-                    op=ALU.mult,
+                    out=w_cols, in0=w_cols, in1=ms_tiles[s // 2][:, pass_columns(s)], op=ALU.mult
                 )
 
             def maximum(pt, q):
@@ -254,6 +282,9 @@ def tile_xmem_pa_k_kernel(
                 similarities(s)
                 if s == 0:
                     sum_b()
+                    spread_shrinkage(0)
+                if s % 2 == 0 and s // 2 + 1 < PAIRS:
+                    spread_shrinkage(s // 2 + 1)
                 for g in to_copy:
                     copy_values(g, 0, nc.scalar.copy)
                 empty_on_vector(0, s)
@@ -400,7 +431,7 @@ def tile_xmem_pa_k_kernel(
             )
             mem = [mem0, mem1]
             for h in range(VAL // HALF_VAL):
-                bank = psum_val.tile([P, 2, PIX], F32)
+                bank = psum_val.tile([P, 2, PIX], F32, tag="val")
                 for q in range(2):
                     channels = slice((2 * h + q) * P, (2 * h + q + 1) * P)
                     for pt in range(PIX_TILES):

@@ -25,12 +25,16 @@ K_PASS = 4 * P
 PASSES = SLOTS // K_PASS
 PAIR = 2 * K_PASS
 PAIRS = SLOTS // PAIR
-MS_ROWS = 2 * PASSES
+VECTOR_REST = 4
+VSHARE = 4
+GSHARE = 4
+LAG = 2
 EXP_SCALE = 2.0 / math.sqrt(CK)
 
-EARLY_COUNT = 9
-EARLY = [4 + (i * (PASSES - 4)) // EARLY_COUNT for i in range(EARLY_COUNT)]
-EARLY_STEP = [3 + (i * (PASSES - 5)) // EARLY_COUNT for i in range(EARLY_COUNT)]
+EARLY = list(range(4, PASSES, 2))
+EARLY_HALVES = [(g, h) for g in EARLY for h in range(2)]
+FIRST_EARLY = 3
+HALF_STEPS = [s for s in range(FIRST_EARLY, PASSES) if s % 4 != 2]
 LATE = [g for g in range(PASSES) if g not in EARLY]
 
 FLOPS = 2 * SLOTS * PIX * (2 * CK + VAL)
@@ -55,7 +59,7 @@ def tile_xmem_pa_k_kernel(
     mk_dram = memory_key.rearrange("b c t h w -> (b c) (t h w)")
     m2_dram = mk_sq.rearrange("b c t h w -> (b c) (t h w)")
     ms_dram = memory_shrinkage.rearrange("b o t h w -> (b o t h w)").rearrange(
-        "(r n) -> r n", r=MS_ROWS
+        "(s n) -> s n", s=PASSES
     )
     mv_dram = memory_value.rearrange("b o c t h w -> (b o c) (t h w)").rearrange(
         "(q r) n -> r q n", r=P
@@ -65,11 +69,11 @@ def tile_xmem_pa_k_kernel(
     with ExitStack() as whole:
         whole.enter_context(tc.manual_schedule())
         const = whole.enter_context(tc.tile_pool(name="const", bufs=1))
-        sim_pool = whole.enter_context(tc.tile_pool(name="sim", bufs=1))
+        wide_pool = whole.enter_context(tc.tile_pool(name="wide", bufs=PIX_TILES * PAIRS))
         early_pool = whole.enter_context(tc.tile_pool(name="early", bufs=1))
-        raw_pool = whole.enter_context(tc.tile_pool(name="raw", bufs=4))
-        grouped_pool = whole.enter_context(tc.tile_pool(name="grouped", bufs=4))
+        raw_pool = whole.enter_context(tc.tile_pool(name="raw", bufs=3))
         e_grouped_pool = whole.enter_context(tc.tile_pool(name="e_grouped", bufs=3))
+        e0_pool = whole.enter_context(tc.tile_pool(name="e0", bufs=3))
         psum_val = whole.enter_context(tc.psum_pool(name="psum_val", bufs=4))
 
         raws = {}
@@ -81,76 +85,81 @@ def tile_xmem_pa_k_kernel(
             nc.sync.dma_start(out=raw[:], in_=mv_dram[:, :, g * K_PASS : (g + 1) * K_PASS])
             raws[g] = raw
 
-        def transpose_values(g):
-            banks = []
-            for h in range(VAL // HALF_VAL):
-                bank = psum_val.tile([P, 2, HALF_VAL], F32, tag="val")
-                for u in range(2):
-                    for q in range(HALF_VAL // P):
-                        words = raws[g][:, h * (HALF_VAL // P) + q, :].bitcast(F32)
-                        nc.tensor.transpose(
-                            bank[:, u, q * P : (q + 1) * P],
-                            words[:, u : 2 * P : 2],
-                            ident_f32[:],
-                        )
-                banks.append(bank)
-            mv_banks[g] = banks
+        def transpose_values(g, h):
+            bank = psum_val.tile([P, 2, HALF_VAL], F32, tag="val")
+            for u in range(2):
+                for q in range(HALF_VAL // P):
+                    words = raws[g][:, h * (HALF_VAL // P) + q, :].bitcast(F32)
+                    nc.tensor.transpose(
+                        bank[:, u, q * P : (q + 1) * P],
+                        words[:, u : 2 * P : 2],
+                        ident_f32[:],
+                    )
+            mv_banks[(g, h)] = bank
 
         def copy_values(g, h, copy):
             pairs = mv_grouped[g][:].rearrange("i (v u) -> i v u", u=2)
             copy(
                 out=pairs[:, h * HALF_VAL : (h + 1) * HALF_VAL, :],
-                in_=mv_banks[g][h][:].rearrange("i u v -> i v u"),
+                in_=mv_banks[(g, h)][:].rearrange("i u v -> i v u"),
             )
 
-        w = [
-            [sim_pool.tile([P, PAIR], F32, name="w%d_%d" % (pt, q)) for q in range(PAIRS)]
-            for pt in range(PIX_TILES)
-        ]
+        w = {}
+
+        def wide_tile():
+            tile = wide_pool.tile([P, PAIR], F32, tag="wide", align_bytes=64)
+            return tile
+
         for g in EARLY:
             mv_grouped[g] = early_pool.tile([P, 2 * VAL], F32, name="early%d" % g, align_bytes=64)
 
+        def copy_values_on_scalar(g):
+            for h in range(VAL // HALF_VAL):
+                copy_values(g, h, nc.scalar.copy)
+
+        e_sb = {}
+        shift = const.tile([P, PIX_TILES], F32)
+        e_sums = const.tile([P, PIX_TILES, PAIRS + 1], F32)
+        nc.vector.memset(e_sums[:, 0, PAIRS : PAIRS + 1], 0.0)
+
+        def exponential(pool, pt, q, cols, column):
+            if (pt, q) not in e_sb:
+                e_sb[(pt, q)] = pool.tile([P, PAIR], BF16, name="e")
+            nc.scalar.activation(
+                out=e_sb[(pt, q)][:, cols],
+                in_=w[(pt, q)][:, cols],
+                func=ACT.Exp,
+                bias=shift[:, pt : pt + 1],
+                scale=EXP_SCALE,
+                accum_out=e_sums[:, pt, column : column + 1],
+            )
+
         with ExitStack() as phase1:
-            stream = phase1.enter_context(tc.tile_pool(name="stream", bufs=3))
+            key_pool = phase1.enter_context(tc.tile_pool(name="keys", bufs=4))
+            ms_pool = phase1.enter_context(tc.tile_pool(name="ms", bufs=4))
             psum_sim = phase1.enter_context(tc.psum_pool(name="psum_sim", bufs=4))
 
             keys = {}
 
             def load_keys(q):
                 slots = slice(q * PAIR, (q + 1) * PAIR)
-                mk_sb = stream.tile([P, PAIR], BF16)
+                mk_sb = key_pool.tile([P, PAIR], BF16)
                 nc.sync.dma_start(out=mk_sb[:], in_=mk_dram[:, slots])
-                m2_sb = stream.tile([P, PAIR], BF16)
+                m2_sb = key_pool.tile([P, PAIR], BF16)
                 nc.sync.dma_start(out=m2_sb[:], in_=m2_dram[:, slots])
                 keys[q] = (mk_sb, m2_sb)
 
-            ms_tiles = {}
-
-            def spread_shrinkage(q):
-                bank = psum_val.tile([P, PAIR], BF16, tag="val")
-                for s in (2 * q, 2 * q + 1):
-                    for u in range(2):
-                        for h in range(2):
-                            first = (s % 2) * K_PASS + u * 2 * P + h * P
-                            column = u * MS_ROWS + 2 * s + h
-                            nc.tensor.transpose(
-                                bank[:, first : first + P],
-                                ms_cols[:, column : column + 1].to_broadcast([P, P]),
-                                ident_bf16[:],
-                            )
-                ms_sb = stream.tile([P, PAIR], BF16)
-                nc.scalar.copy(out=ms_sb[:], in_=bank[:])
-                ms_tiles[q] = ms_sb
-
-            ms_rows = const.tile([P, 2 * P], BF16)
-            for u in range(2):
-                nc.sync.dma_start(out=ms_rows[u * MS_ROWS : (u + 1) * MS_ROWS, :], in_=ms_dram)
-            qs_sb = const.tile([P, PIX], BF16)
-            nc.sync.dma_start(out=qs_sb[:], in_=qs_dram)
-            qe_sb = const.tile([P, PIX], BF16)
-            nc.sync.dma_start(out=qe_sb[:], in_=qe_dram)
             qk_sb = const.tile([P, PIX], BF16)
             nc.sync.dma_start(out=qk_sb[:], in_=qk_dram)
+            qe_sb = const.tile([P, PIX], BF16)
+            nc.sync.dma_start(out=qe_sb[:], in_=qe_dram)
+            ms_rows = const.tile([P, K_PASS], BF16)
+            for copy in range(P // PASSES):
+                nc.sync.dma_start(
+                    out=ms_rows[copy * PASSES : (copy + 1) * PASSES, :], in_=ms_dram
+                )
+            qs_sb = const.tile([P, PIX], BF16)
+            nc.sync.dma_start(out=qs_sb[:], in_=qs_dram)
             load_keys(0)
             load_keys(1)
 
@@ -159,47 +168,54 @@ def tile_xmem_pa_k_kernel(
             nc.scalar.activation(out=warm[:], in_=warm[:], func=ACT.Exp)
             ident_f32 = const.tile([P, P], F32)
             make_identity(nc, ident_f32[:])
-            ident_bf16 = const.tile([P, P], BF16)
-            make_identity(nc, ident_bf16[:])
 
-            ms_pairs = const.tile([P, P], BF16)
-            for u in range(2):
-                rows = slice(u * MS_ROWS, (u + 1) * MS_ROWS)
-                nc.vector.tensor_copy(
-                    out=ms_pairs[rows, :].rearrange("r (i e) -> r i e", e=2),
-                    in_=ms_rows[rows, :].rearrange("r (i u e) -> r u i e", u=2, e=2)[:, u],
-                )
-            ms_bank = psum_val.tile([P, P], BF16, tag="val")
-            nc.tensor.transpose(ms_bank[:], ms_pairs[:], ident_bf16[:])
-            ms_cols = const.tile([P, P], BF16)
-            nc.vector.tensor_copy(out=ms_cols[:], in_=ms_bank[:])
-
-            qe_half = const.tile([P, PIX], BF16)
-            nc.vector.tensor_scalar(
-                out=qe_half[:], in0=qe_sb[:], scalar1=-0.5, scalar2=None, op0=ALU.mult
-            )
             qk_sq = const.tile([P, PIX], F32)
             nc.vector.tensor_tensor(out=qk_sq[:], in0=qk_sb[:], in1=qk_sb[:], op=ALU.mult)
             b_terms = const.tile([P, PIX], F32)
             nc.vector.tensor_tensor(out=b_terms[:], in0=qk_sq[:], in1=qe_sb[:], op=ALU.mult)
-            b_sum = const.tile([P, PIX_TILES], F32)
-            b_minus = const.tile([P, PIX_TILES], F32)
-
-            def sum_b():
-                b_bank = psum_sim.tile([P, PIX_TILES, P], F32, tag="u")
-                for pt in range(PIX_TILES):
-                    nc.tensor.transpose(
-                        b_bank[:, pt, :], b_terms[:, pt * P : (pt + 1) * P], ident_f32[:]
-                    )
-                nc.vector.reduce_sum(out=b_sum[:], in_=b_bank[:], axis=AXIS.X)
-                nc.vector.tensor_scalar(
-                    out=b_minus[:], in0=b_sum[:], scalar1=-0.5, scalar2=None, op0=ALU.mult
+            qe_half = const.tile([P, PIX], BF16)
+            nc.vector.tensor_scalar(
+                out=qe_half[:], in0=qe_sb[:], scalar1=-0.5, scalar2=None, op0=ALU.mult
+            )
+            b_bank = psum_sim.tile([P, PIX_TILES, P], F32, tag="u")
+            for pt in range(PIX_TILES):
+                nc.tensor.transpose(
+                    b_bank[:, pt, :], b_terms[:, pt * P : (pt + 1) * P], ident_f32[:]
                 )
+            b_sum = const.tile([P, PIX_TILES], F32)
+            nc.vector.reduce_sum(out=b_sum[:], in_=b_bank[:], axis=AXIS.X)
+            b_minus = const.tile([P, PIX_TILES], F32)
+            nc.vector.tensor_scalar(
+                out=b_minus[:], in0=b_sum[:], scalar1=-0.5, scalar2=None, op0=ALU.mult
+            )
+
+            ms_bank = psum_val.tile([P, 2, P], F32, tag="val")
+            for u in range(2):
+                nc.tensor.transpose(
+                    ms_bank[:, u, :], ms_rows[:].bitcast(F32)[:, u::2], ident_f32[:]
+                )
+            ms_words = const.tile([P, 2, PASSES], F32)
+            nc.vector.tensor_copy(out=ms_words[:], in_=ms_bank[:, :, 0:PASSES])
+
+            ms_tiles = {}
+
+            def spread_shrinkage(q):
+                bank = psum_val.tile([P, 2, 2, P], F32, tag="val")
+                for s in range(2):
+                    for u in range(2):
+                        column = ms_words[:, u, 2 * q + s : 2 * q + s + 1]
+                        nc.tensor.transpose(
+                            bank[:, s, u, :], column.to_broadcast([P, P]), ident_f32[:]
+                        )
+                ms_sb = ms_pool.tile([P, PAIR], BF16)
+                nc.scalar.copy(
+                    out=ms_sb[:].bitcast(F32), in_=bank[:].rearrange("p s u i -> p (s u i)")
+                )
+                ms_tiles[q] = ms_sb
 
             u_banks = {}
             pair_max = const.tile([P, PIX_TILES, PAIRS], F32)
             w_max = const.tile([P, PIX_TILES], F32)
-            shift = const.tile([P, PIX_TILES], F32)
 
             def by_word(ap):
                 return ap.rearrange("p (i u e) -> p u i e", u=2, e=2)
@@ -207,31 +223,30 @@ def tile_xmem_pa_k_kernel(
             def pass_columns(s):
                 return slice((s % 2) * K_PASS, (s % 2 + 1) * K_PASS)
 
-            def similarities(s):
+            def similarities(pt, s):
                 mk_sb, m2_sb = keys[s // 2]
                 cols = pass_columns(s)
-                for pt in range(PIX_TILES):
-                    pixels = slice(pt * P, (pt + 1) * P)
-                    u = psum_sim.tile([P, K_PASS], F32, tag="u")
-                    nc.tensor.matmul(
-                        u[:],
-                        lhsT=qs_sb[:, pixels],
-                        rhs=by_word(mk_sb[:, cols]),
-                        start=True,
-                        stop=False,
-                    )
-                    nc.tensor.matmul(
-                        u[:],
-                        lhsT=qe_half[:, pixels],
-                        rhs=by_word(m2_sb[:, cols]),
-                        start=False,
-                        stop=True,
-                    )
-                    u_banks[(pt, s)] = u
+                pixels = slice(pt * P, (pt + 1) * P)
+                u = psum_sim.tile([P, K_PASS], F32, tag="u")
+                nc.tensor.matmul(
+                    u[:],
+                    lhsT=qs_sb[:, pixels],
+                    rhs=by_word(mk_sb[:, cols]),
+                    start=True,
+                    stop=False,
+                )
+                nc.tensor.matmul(
+                    u[:],
+                    lhsT=qe_half[:, pixels],
+                    rhs=by_word(m2_sb[:, cols]),
+                    start=False,
+                    stop=True,
+                )
+                u_banks[(pt, s)] = u
 
             def empty_on_vector(pt, s):
                 nc.vector.scalar_tensor_tensor(
-                    out=w[pt][s // 2][:, pass_columns(s)],
+                    out=w[(pt, s // 2)][:, pass_columns(s)],
                     in0=u_banks[(pt, s)][:],
                     scalar=b_minus[:, pt : pt + 1],
                     in1=ms_tiles[s // 2][:, pass_columns(s)],
@@ -240,7 +255,7 @@ def tile_xmem_pa_k_kernel(
                 )
 
             def empty_on_scalar(pt, s):
-                w_cols = w[pt][s // 2][:, pass_columns(s)]
+                w_cols = w[(pt, s // 2)][:, pass_columns(s)]
                 nc.scalar.activation(
                     out=w_cols,
                     in_=u_banks[(pt, s)][:],
@@ -252,9 +267,7 @@ def tile_xmem_pa_k_kernel(
                 )
 
             def maximum(pt, q):
-                nc.vector.reduce_max(
-                    out=pair_max[:, pt, q : q + 1], in_=w[pt][q][:], axis=AXIS.X
-                )
+                nc.vector.reduce_max(out=pair_max[:, pt, q : q + 1], in_=w[(pt, q)][:], axis=AXIS.X)
 
             def find_shift(pt):
                 nc.vector.reduce_max(
@@ -268,75 +281,89 @@ def tile_xmem_pa_k_kernel(
                     op0=ALU.mult,
                 )
 
-            to_copy = []
-            for s in range(PASSES):
+            spread_shrinkage(0)
+            for s in range(PASSES + LAG):
+                p = s - LAG
                 if s % 2 == 0 and s // 2 + 2 < PAIRS:
                     load_keys(s // 2 + 2)
-                for g, step in zip(EARLY, EARLY_STEP):
-                    if s == max(0, step - 3):
+                if s + 3 in HALF_STEPS:
+                    g, h = EARLY_HALVES[HALF_STEPS.index(s + 3)]
+                    if h == 0:
                         load_values(g)
-                if s == PASSES - 4:
+                if s == PASSES - 1:
+                    for g, h in EARLY_HALVES[len(HALF_STEPS) :]:
+                        if h == 0:
+                            load_values(g)
+                if s == PASSES:
                     load_values(0)
-                if s == PASSES - 2:
                     load_values(1)
-                similarities(s)
-                if s == 0:
-                    sum_b()
-                    spread_shrinkage(0)
+
+                if s % 2 == 0:
+                    if s < PASSES:
+                        w[(0, s // 2)] = wide_tile()
+                    if p >= 0:
+                        w[(1, p // 2)] = wide_tile()
+
+                if s < PASSES:
+                    similarities(0, s)
+                if p >= 0:
+                    similarities(1, p)
+
+                if s < PASSES:
+                    if s % GSHARE == 2 and s < PASSES - 4:
+                        empty_on_scalar(0, s)
+                    else:
+                        empty_on_vector(0, s)
+                if p >= 0:
+                    if p < PASSES - LAG:
+                        empty_on_scalar(1, p)
+                    else:
+                        empty_on_vector(1, p)
                 if s % 2 == 0 and s // 2 + 1 < PAIRS:
                     spread_shrinkage(s // 2 + 1)
-                for g in to_copy:
-                    copy_values(g, 0, nc.scalar.copy)
-                empty_on_vector(0, s)
-                if s >= PASSES - 2:
-                    empty_on_vector(1, s)
-                else:
-                    empty_on_scalar(1, s)
-                for g in to_copy:
-                    copy_values(g, 1, nc.scalar.copy)
-                to_copy = []
-                for g, step in zip(EARLY, EARLY_STEP):
-                    if s == step:
-                        transpose_values(g)
-                        to_copy.append(g)
-                if s % 2 == 0 and s >= 2:
+                if s - 1 in HALF_STEPS:
+                    copy_values(*EARLY_HALVES[HALF_STEPS.index(s - 1)], nc.scalar.copy)
+                if s in HALF_STEPS:
+                    transpose_values(*EARLY_HALVES[HALF_STEPS.index(s)])
+
+                if s % 2 == 0 and 2 <= s < PASSES:
                     maximum(0, s // 2 - 1)
-                if s % 2 == 1 and s >= 3:
-                    maximum(1, (s - 3) // 2)
-            for g in to_copy:
-                copy_values(g, 0, nc.scalar.copy)
-                copy_values(g, 1, nc.scalar.copy)
-            for pt in range(PIX_TILES):
-                maximum(pt, PAIRS - 1)
-                find_shift(pt)
+                if s % 2 == 1 and p >= 3:
+                    maximum(1, (p - 3) // 2)
+                if s == PASSES - 1:
+                    maximum(0, PAIRS - 1)
+                    find_shift(0)
+
+            rest = EARLY_HALVES[len(HALF_STEPS) :] + [(0, 0), (0, 1), (1, 0), (1, 1)]
+            for g in (0, 1):
+                mv_grouped[g] = wide_tile()
+            for i in range(len(rest)):
+                transpose_values(*rest[i])
+                if i == 1:
+                    exponential(e0_pool, 0, 0, slice(0, PAIR), 0)
+                if i == 4:
+                    exponential(e0_pool, 0, 1, slice(0, PAIR), 1)
+                if i < len(rest) - VECTOR_REST:
+                    copy_values(*rest[i], nc.scalar.copy)
+            maximum(1, PAIRS - 1)
+            find_shift(1)
+            for i in range(len(rest) - VECTOR_REST, len(rest)):
+                copy_values(*rest[i], nc.vector.tensor_copy)
 
         psum_acc = whole.enter_context(tc.psum_pool(name="psum_acc", bufs=1))
         acc = [psum_acc.tile([P, VAL], F32, name="acc%d" % pt) for pt in range(PIX_TILES)]
-        e_sums = const.tile([P, PIX_TILES, PAIRS + 1], F32)
 
         with ExitStack() as phase:
-            e_pool = phase.enter_context(tc.tile_pool(name="e", bufs=3))
-            e_mx_pool = phase.enter_context(tc.tile_pool(name="e_mx", bufs=3))
-            mv_mx_pool = phase.enter_context(tc.tile_pool(name="mv_mx", bufs=4))
+            e1_pool = phase.enter_context(tc.tile_pool(name="e1", bufs=3))
+            e_mx_pool = phase.enter_context(tc.tile_pool(name="e_mx", bufs=4))
+            mv_mx_pool = phase.enter_context(tc.tile_pool(name="mv_mx", bufs=5))
             psum_e = phase.enter_context(tc.psum_pool(name="psum_e", bufs=2))
+            e_pools = [e0_pool, e1_pool]
 
-            e_sb = {}
             e_banks = {}
             e_grouped = {}
             e_codes = {}
             mv_codes = {}
-
-            def exponential(pt, q, cols, column):
-                if (pt, q) not in e_sb:
-                    e_sb[(pt, q)] = e_pool.tile([P, PAIR], BF16, name="e%d" % pt, tag="e%d" % pt)
-                nc.scalar.activation(
-                    out=e_sb[(pt, q)][:, cols],
-                    in_=w[pt][q][:, cols],
-                    func=ACT.Exp,
-                    bias=shift[:, pt : pt + 1],
-                    scale=EXP_SCALE,
-                    accum_out=e_sums[:, pt, column : column + 1],
-                )
 
             def transpose_e(g):
                 q, s = divmod(g, 2)
@@ -380,40 +407,45 @@ def tile_xmem_pa_k_kernel(
                         stop=(g == PASSES - 1),
                     )
 
-            loads = LATE[2:]
-            for k in range(-2, PASSES + 3):
-                if k >= -2 and loads and k + 5 >= loads[0]:
-                    load_values(loads.pop(0))
-                if 0 <= k < PASSES:
+            exponential(e1_pool, 1, 0, slice(0, K_PASS), 0)
+            exponential(e1_pool, 1, 0, slice(K_PASS, PAIR), PAIRS)
+            load_values(2)
+            load_values(3)
+            loads = LATE[4:]
+            for k in range(PASSES + 4):
+                if loads and k + 5 >= loads[0]:
+                    load_values(loads[0])
+                    loads = loads[1:]
+                if k < PASSES:
                     transpose_e(k)
                 if k + 2 in LATE:
-                    transpose_values(k + 2)
-                if k + 1 in LATE:
-                    mv_grouped[k + 1] = grouped_pool.tile([P, 2 * VAL], F32, align_bytes=64, name="mv_four")
-                    share = LATE.index(k + 1) % 2 == 1
+                    transpose_values(k + 2, 0)
+                    transpose_values(k + 2, 1)
+                if k % 2 == 0 and k >= 4:
+                    readout(k - 4)
+                    readout(k - 3)
+
+                on_vector = False
+                if k >= 1 and k + 1 in LATE:
+                    mv_grouped[k + 1] = wide_tile()
+                    on_vector = LATE.index(k + 1) % VSHARE == 0
                     copy_values(k + 1, 0, nc.scalar.copy)
-                    if not share:
+                    if not on_vector:
                         copy_values(k + 1, 1, nc.scalar.copy)
-                if k == -1:
-                    first, second = slice(0, K_PASS), slice(K_PASS, PAIR)
-                    for pt in range(PIX_TILES):
-                        exponential(pt, 0, first, 0)
-                        exponential(pt, 0, second, PAIRS)
-                    exponential(0, 1, slice(0, PAIR), 1)
-                if k >= 0 and (k + 3) // 2 < PAIRS:
-                    exponential((k + 1) % 2, (k + 3) // 2, slice(0, PAIR), (k + 3) // 2)
+                if (k + 3) // 2 < PAIRS:
+                    pt = (k + 1) % 2
+                    exponential(e_pools[pt], pt, (k + 3) // 2, slice(0, PAIR), (k + 3) // 2)
+
                 if 1 <= k <= PASSES:
                     copy_e(k - 1)
-                if k + 1 in LATE and share:
+                if on_vector:
                     copy_values(k + 1, 1, nc.vector.tensor_copy)
                 if 2 <= k <= PASSES + 1:
                     e_codes[k - 2] = quantise(
                         e_grouped[k - 2][:].rearrange("i p u -> i (p u)"), PIX, e_mx_pool
                     )
-                if 1 <= k <= PASSES:
-                    mv_codes[k - 1] = quantise(mv_grouped[k - 1][:], VAL, mv_mx_pool)
-                if 3 <= k <= PASSES + 2:
-                    readout(k - 3)
+                if k < PASSES:
+                    mv_codes[k] = quantise(mv_grouped[k][:], VAL, mv_mx_pool)
 
         with tc.tile_pool(name="tail", bufs=2) as tail:
             total = const.tile([P, PIX_TILES], F32)

@@ -113,10 +113,6 @@ def tile_xmem_pa_k_kernel(
         for g in EARLY:
             mv_grouped[g] = early_pool.tile([P, 2 * VAL], F32, name="early%d" % g, align_bytes=64)
 
-        def copy_values_on_scalar(g):
-            for h in range(VAL // HALF_VAL):
-                copy_values(g, h, nc.scalar.copy)
-
         e_sb = {}
         shift = const.tile([P, PIX_TILES], F32)
         e_sums = const.tile([P, PIX_TILES, PAIRS + 1], F32)
@@ -411,35 +407,37 @@ def tile_xmem_pa_k_kernel(
             exponential(e1_pool, 1, 0, slice(K_PASS, PAIR), PAIRS)
             load_values(2)
             load_values(3)
+            halves = {k: [(k + 2, 0), (k + 2, 1)] for k in range(2)}
+            for g in LATE[4:]:
+                halves[g - 3] = [(g, 0)]
+                halves[g - 2] = [(g, 1)]
+            on_vector = [(g, 1) for g in LATE if LATE.index(g) % VSHARE == 0]
             loads = LATE[4:]
-            for k in range(PASSES + 4):
-                if loads and k + 5 >= loads[0]:
+            for k in range(PASSES + 3):
+                if loads and k + 6 >= loads[0]:
                     load_values(loads[0])
                     loads = loads[1:]
                 if k < PASSES:
                     transpose_e(k)
-                if k + 2 in LATE:
-                    transpose_values(k + 2, 0)
-                    transpose_values(k + 2, 1)
-                if k % 2 == 0 and k >= 4:
-                    readout(k - 4)
+                for half in halves.get(k, []):
+                    transpose_values(*half)
+                if k >= 3:
                     readout(k - 3)
 
-                on_vector = False
-                if k >= 1 and k + 1 in LATE:
-                    mv_grouped[k + 1] = wide_tile()
-                    on_vector = LATE.index(k + 1) % VSHARE == 0
-                    copy_values(k + 1, 0, nc.scalar.copy)
-                    if not on_vector:
-                        copy_values(k + 1, 1, nc.scalar.copy)
+                for g, h in halves.get(k - 1, []):
+                    if h == 0:
+                        mv_grouped[g] = wide_tile()
+                    if (g, h) not in on_vector:
+                        copy_values(g, h, nc.scalar.copy)
                 if (k + 3) // 2 < PAIRS:
                     pt = (k + 1) % 2
                     exponential(e_pools[pt], pt, (k + 3) // 2, slice(0, PAIR), (k + 3) // 2)
 
                 if 1 <= k <= PASSES:
                     copy_e(k - 1)
-                if on_vector:
-                    copy_values(k + 1, 1, nc.vector.tensor_copy)
+                for half in halves.get(k - 1, []):
+                    if half in on_vector:
+                        copy_values(*half, nc.vector.tensor_copy)
                 if 2 <= k <= PASSES + 1:
                     e_codes[k - 2] = quantise(
                         e_grouped[k - 2][:].rearrange("i p u -> i (p u)"), PIX, e_mx_pool
@@ -447,32 +445,35 @@ def tile_xmem_pa_k_kernel(
                 if k < PASSES:
                     mv_codes[k] = quantise(mv_grouped[k][:], VAL, mv_mx_pool)
 
-        with tc.tile_pool(name="tail", bufs=2) as tail:
+        with tc.tile_pool(name="tail", bufs=VAL_TILES) as tail:
+            result_banks = []
             total = const.tile([P, PIX_TILES], F32)
             nc.vector.reduce_sum(out=total[:], in_=e_sums[:], axis=AXIS.X)
             inv_total = const.tile([P, PIX_TILES], F32)
             nc.vector.reciprocal(out=inv_total[:], in_=total[:])
 
-            mem0 = tail.tile([P, VAL], F32)
-            nc.vector.tensor_scalar(
-                out=mem0[:], in0=acc[0][:], scalar1=inv_total[:, 0:1], scalar2=None, op0=ALU.mult
-            )
-            mem1 = tail.tile([P, VAL], F32)
-            nc.scalar.activation(
-                out=mem1[:], in_=acc[1][:], func=ACT.Copy, scale=inv_total[:, 1:2]
-            )
-            mem = [mem0, mem1]
-            for h in range(VAL // HALF_VAL):
-                bank = psum_val.tile([P, 2, PIX], F32, tag="val")
-                for q in range(2):
-                    channels = slice((2 * h + q) * P, (2 * h + q + 1) * P)
-                    for pt in range(PIX_TILES):
-                        nc.tensor.transpose(
-                            bank[:, q, pt * P : (pt + 1) * P], mem[pt][:, channels], ident_f32[:]
-                        )
-                result = tail.tile([P, 2, PIX], F32)
-                if h == 0:
-                    nc.vector.tensor_copy(out=result[:], in_=bank[:])
+            for c in range(VAL_TILES):
+                channels = slice(c * P, (c + 1) * P)
+                mem0 = tail.tile([P, P], F32)
+                nc.vector.tensor_scalar(
+                    out=mem0[:],
+                    in0=acc[0][:, channels],
+                    scalar1=inv_total[:, 0:1],
+                    scalar2=None,
+                    op0=ALU.mult,
+                )
+                mem1 = tail.tile([P, P], F32)
+                nc.scalar.activation(
+                    out=mem1[:], in_=acc[1][:, channels], func=ACT.Copy, scale=inv_total[:, 1:2]
+                )
+                bank = psum_val.tile([P, PIX], F32, tag="val")
+                nc.tensor.transpose(bank[:, 0:P], mem0[:], ident_f32[:])
+                nc.tensor.transpose(bank[:, P:PIX], mem1[:], ident_f32[:])
+                result_banks.append(bank)
+            for c in range(VAL_TILES):
+                result = tail.tile([P, PIX], F32)
+                if c % 2 == 0:
+                    nc.vector.tensor_copy(out=result[:], in_=result_banks[c][:])
                 else:
-                    nc.scalar.copy(out=result[:], in_=bank[:])
-                nc.sync.dma_start(out=out_dram[:, 2 * h : 2 * h + 2, :], in_=result[:])
+                    nc.scalar.copy(out=result[:], in_=result_banks[c][:])
+                nc.sync.dma_start(out=out_dram[:, c, :], in_=result[:])

@@ -150,10 +150,8 @@ def tile_xmem_pa_k_kernel(
             qe_sb = const.tile([P, PIX], BF16)
             nc.sync.dma_start(out=qe_sb[:], in_=qe_dram)
             ms_rows = const.tile([P, K_PASS], BF16)
-            for copy in range(P // PASSES):
-                nc.sync.dma_start(
-                    out=ms_rows[copy * PASSES : (copy + 1) * PASSES, :], in_=ms_dram
-                )
+            nc.vector.memset(ms_rows[:], 0.0)
+            nc.sync.dma_start(out=ms_rows[0:PASSES, :], in_=ms_dram)
             qs_sb = const.tile([P, PIX], BF16)
             nc.sync.dma_start(out=qs_sb[:], in_=qs_dram)
             load_keys(0)
@@ -383,8 +381,8 @@ def tile_xmem_pa_k_kernel(
                 e_grouped[g] = e_four
 
             def quantise(words, columns, pool):
-                codes = pool.tile([P, columns], U32, align_bytes=64)
-                scales = pool.tile([P, columns], U8, align_bytes=64)
+                codes = pool.tile([P, columns], U32, align_bytes=256)
+                scales = pool.tile([P, columns], U8, align_bytes=256)
                 nc.vector.quantize_mx(
                     out=codes[:].bitcast(FP8X4), scales=scales[:], in_=words.bitcast(BF16)
                 )

@@ -225,34 +225,40 @@ def tile_xmem_pa_k_kernel(
                 nc.tensor.matmul(
                     u[:],
                     lhsT=qs_sb[:, pixels],
-                    rhs=by_word(mk_sb[:, cols]),
+                    rhs=mk_sb[:, cols],
                     start=True,
                     stop=False,
                 )
                 nc.tensor.matmul(
                     u[:],
                     lhsT=qe_half[:, pixels],
-                    rhs=by_word(m2_sb[:, cols]),
+                    rhs=m2_sb[:, cols],
                     start=False,
                     stop=True,
                 )
                 u_banks[(pt, s)] = u
 
             def empty_on_vector(pt, s):
-                nc.vector.scalar_tensor_tensor(
-                    out=w[(pt, s // 2)][:, pass_columns(s)],
-                    in0=u_banks[(pt, s)][:],
-                    scalar=b_minus[:, pt : pt + 1],
-                    in1=ms_tiles[s // 2][:, pass_columns(s)],
-                    op0=ALU.add,
-                    op1=ALU.mult,
-                )
+                for half in range(2):
+                    first = (s % 2) * K_PASS + half * 2 * P
+                    nc.vector.scalar_tensor_tensor(
+                        out=w[(pt, s // 2)][:, first : first + 2 * P].rearrange(
+                            "p (i e) -> p i e", e=2
+                        ),
+                        in0=by_word(u_banks[(pt, s)][:])[:, half],
+                        scalar=b_minus[:, pt : pt + 1],
+                        in1=ms_tiles[s // 2][:, first : first + 2 * P].rearrange(
+                            "p (i e) -> p i e", e=2
+                        ),
+                        op0=ALU.add,
+                        op1=ALU.mult,
+                    )
 
             def empty_on_scalar(pt, s):
                 w_cols = w[(pt, s // 2)][:, pass_columns(s)]
                 nc.scalar.activation(
-                    out=w_cols,
-                    in_=u_banks[(pt, s)][:],
+                    out=w_cols.rearrange("p (u i e) -> p u i e", u=2, e=2),
+                    in_=by_word(u_banks[(pt, s)][:]),
                     func=ACT.Identity,
                     bias=b_minus[:, pt : pt + 1],
                 )

@@ -28,6 +28,7 @@ PAIRS = SLOTS // PAIR
 VECTOR_REST = 4
 VSHARE = 4
 GSHARE = 4
+WARM_MATMULS = 5
 LAG = 2
 EXP_SCALE = 2.0 / math.sqrt(CK)
 
@@ -163,10 +164,17 @@ def tile_xmem_pa_k_kernel(
             ident_f32 = const.tile([P, P], F32)
             make_identity(nc, ident_f32[:])
 
-            qk_sq = const.tile([P, PIX], F32)
-            nc.vector.tensor_tensor(out=qk_sq[:], in0=qk_sb[:], in1=qk_sb[:], op=ALU.mult)
+            zeros = const.tile([P, K_PASS], BF16)
+            nc.vector.memset(zeros[:], 0.0)
+            warm_bank = psum_sim.tile([P, K_PASS], F32, tag="u")
+            for i in range(WARM_MATMULS):
+                nc.tensor.matmul(
+                    warm_bank[:], lhsT=zeros[:, 0:P], rhs=zeros[:], start=True, stop=True
+                )
+
             b_terms = const.tile([P, PIX], F32)
-            nc.vector.tensor_tensor(out=b_terms[:], in0=qk_sq[:], in1=qe_sb[:], op=ALU.mult)
+            nc.vector.tensor_tensor(out=b_terms[:], in0=qk_sb[:], in1=qk_sb[:], op=ALU.mult)
+            nc.vector.tensor_tensor(out=b_terms[:], in0=b_terms[:], in1=qe_sb[:], op=ALU.mult)
             qe_half = const.tile([P, PIX], BF16)
             nc.vector.tensor_scalar(
                 out=qe_half[:], in0=qe_sb[:], scalar1=-0.5, scalar2=None, op0=ALU.mult
@@ -418,7 +426,7 @@ def tile_xmem_pa_k_kernel(
             on_vector = [(g, 1) for g in LATE if LATE.index(g) % VSHARE == 0]
             loads = LATE[4:]
             for k in range(PASSES + 3):
-                if loads and k + 6 >= loads[0]:
+                if loads and k + 7 >= loads[0]:
                     load_values(loads[0])
                     loads = loads[1:]
                 if k < PASSES:

@@ -28,11 +28,11 @@ PAIRS = SLOTS // PAIR
 VECTOR_REST = 4
 VSHARE = 4
 GSHARE = 4
-WARM_MATMULS = 5
+WARM_MATMULS = 6
 LAG = 2
 EXP_SCALE = 2.0 / math.sqrt(CK)
 
-EARLY = list(range(4, PASSES, 2))
+EARLY = list(range(6, PASSES, 2))
 EARLY_HALVES = [(g, h) for g in EARLY for h in range(2)]
 FIRST_EARLY = 3
 HALF_STEPS = [s for s in range(FIRST_EARLY, PASSES) if s % 4 != 2]
@@ -72,7 +72,7 @@ def tile_xmem_pa_k_kernel(
         const = whole.enter_context(tc.tile_pool(name="const", bufs=1))
         wide_pool = whole.enter_context(tc.tile_pool(name="wide", bufs=PIX_TILES * PAIRS))
         early_pool = whole.enter_context(tc.tile_pool(name="early", bufs=1))
-        raw_pool = whole.enter_context(tc.tile_pool(name="raw", bufs=3))
+        raw_pool = whole.enter_context(tc.tile_pool(name="raw", bufs=4))
         e_grouped_pool = whole.enter_context(tc.tile_pool(name="e_grouped", bufs=3))
         e0_pool = whole.enter_context(tc.tile_pool(name="e0", bufs=3))
         psum_val = whole.enter_context(tc.psum_pool(name="psum_val", bufs=4))
@@ -146,6 +146,8 @@ def tile_xmem_pa_k_kernel(
                 nc.sync.dma_start(out=m2_sb[:], in_=m2_dram[:, slots])
                 keys[q] = (mk_sb, m2_sb)
 
+            zeros = const.tile([P, K_PASS], BF16)
+            nc.vector.memset(zeros[:], 0.0)
             qk_sb = const.tile([P, PIX], BF16)
             nc.sync.dma_start(out=qk_sb[:], in_=qk_dram)
             qe_sb = const.tile([P, PIX], BF16)
@@ -164,8 +166,6 @@ def tile_xmem_pa_k_kernel(
             ident_f32 = const.tile([P, P], F32)
             make_identity(nc, ident_f32[:])
 
-            zeros = const.tile([P, K_PASS], BF16)
-            nc.vector.memset(zeros[:], 0.0)
             warm_bank = psum_sim.tile([P, K_PASS], F32, tag="u")
             for i in range(WARM_MATMULS):
                 nc.tensor.matmul(
@@ -294,9 +294,9 @@ def tile_xmem_pa_k_kernel(
                 p = s - LAG
                 if s % 2 == 0 and s // 2 + 2 < PAIRS:
                     load_keys(s // 2 + 2)
-                if s + 3 in HALF_STEPS:
-                    g, h = EARLY_HALVES[HALF_STEPS.index(s + 3)]
-                    if h == 0:
+                for step in HALF_STEPS:
+                    g, h = EARLY_HALVES[HALF_STEPS.index(step)]
+                    if h == 0 and s == max(0, step - 5):
                         load_values(g)
                 if s == PASSES - 1:
                     for g, h in EARLY_HALVES[len(HALF_STEPS) :]:
@@ -417,14 +417,14 @@ def tile_xmem_pa_k_kernel(
 
             exponential(e1_pool, 1, 0, slice(0, K_PASS), 0)
             exponential(e1_pool, 1, 0, slice(K_PASS, PAIR), PAIRS)
-            load_values(2)
-            load_values(3)
+            for g in LATE[2:6]:
+                load_values(g)
             halves = {k: [(k + 2, 0), (k + 2, 1)] for k in range(2)}
             for g in LATE[4:]:
-                halves[g - 3] = [(g, 0)]
-                halves[g - 2] = [(g, 1)]
+                for h in range(2):
+                    halves[g - 3 + h] = halves.get(g - 3 + h, []) + [(g, h)]
             on_vector = [(g, 1) for g in LATE if LATE.index(g) % VSHARE == 0]
-            loads = LATE[4:]
+            loads = LATE[6:]
             for k in range(PASSES + 3):
                 if loads and k + 7 >= loads[0]:
                     load_values(loads[0])

@@ -28,7 +28,8 @@ PAIRS = SLOTS // PAIR
 VECTOR_REST = 4
 VSHARE = 4
 GSHARE = 4
-WARM_MATMULS = 6
+WARM_MATMULS = 3
+SCALAR_LAST = 3
 LAG = 2
 EXP_SCALE = 2.0 / math.sqrt(CK)
 
@@ -146,15 +147,13 @@ def tile_xmem_pa_k_kernel(
                 nc.sync.dma_start(out=m2_sb[:], in_=m2_dram[:, slots])
                 keys[q] = (mk_sb, m2_sb)
 
-            zeros = const.tile([P, K_PASS], BF16)
-            nc.vector.memset(zeros[:], 0.0)
+            ms_rows = const.tile([P, K_PASS], BF16)
+            nc.vector.memset(ms_rows[:].bitcast(F32), 0.0)
+            nc.sync.dma_start(out=ms_rows[0:PASSES, :], in_=ms_dram)
             qk_sb = const.tile([P, PIX], BF16)
             nc.sync.dma_start(out=qk_sb[:], in_=qk_dram)
             qe_sb = const.tile([P, PIX], BF16)
             nc.sync.dma_start(out=qe_sb[:], in_=qe_dram)
-            ms_rows = const.tile([P, K_PASS], BF16)
-            nc.vector.memset(ms_rows[:], 0.0)
-            nc.sync.dma_start(out=ms_rows[0:PASSES, :], in_=ms_dram)
             qs_sb = const.tile([P, PIX], BF16)
             nc.sync.dma_start(out=qs_sb[:], in_=qs_dram)
             load_keys(0)
@@ -166,30 +165,13 @@ def tile_xmem_pa_k_kernel(
             ident_f32 = const.tile([P, P], F32)
             make_identity(nc, ident_f32[:])
 
+            zeros = const.tile([P, K_PASS], BF16)
+            nc.vector.memset(zeros[:].bitcast(F32), 0.0)
             warm_bank = psum_sim.tile([P, K_PASS], F32, tag="u")
             for i in range(WARM_MATMULS):
                 nc.tensor.matmul(
                     warm_bank[:], lhsT=zeros[:, 0:P], rhs=zeros[:], start=True, stop=True
                 )
-
-            b_terms = const.tile([P, PIX], F32)
-            nc.vector.tensor_tensor(out=b_terms[:], in0=qk_sb[:], in1=qk_sb[:], op=ALU.mult)
-            nc.vector.tensor_tensor(out=b_terms[:], in0=b_terms[:], in1=qe_sb[:], op=ALU.mult)
-            qe_half = const.tile([P, PIX], BF16)
-            nc.vector.tensor_scalar(
-                out=qe_half[:], in0=qe_sb[:], scalar1=-0.5, scalar2=None, op0=ALU.mult
-            )
-            b_bank = psum_sim.tile([P, PIX_TILES, P], F32, tag="u")
-            for pt in range(PIX_TILES):
-                nc.tensor.transpose(
-                    b_bank[:, pt, :], b_terms[:, pt * P : (pt + 1) * P], ident_f32[:]
-                )
-            b_sum = const.tile([P, PIX_TILES], F32)
-            nc.vector.reduce_sum(out=b_sum[:], in_=b_bank[:], axis=AXIS.X)
-            b_minus = const.tile([P, PIX_TILES], F32)
-            nc.vector.tensor_scalar(
-                out=b_minus[:], in0=b_sum[:], scalar1=-0.5, scalar2=None, op0=ALU.mult
-            )
 
             ms_bank = psum_val.tile([P, 2, P], F32, tag="val")
             for u in range(2):
@@ -197,8 +179,29 @@ def tile_xmem_pa_k_kernel(
                     ms_bank[:, u, :], ms_rows[:].bitcast(F32)[:, u::2], ident_f32[:]
                 )
             ms_words = const.tile([P, 2, PASSES], F32)
-            nc.vector.tensor_copy(out=ms_words[:], in_=ms_bank[:, :, 0:PASSES])
 
+            b_terms = const.tile([P, PIX], F32)
+            nc.vector.tensor_tensor(out=b_terms[:], in0=qk_sb[:], in1=qk_sb[:], op=ALU.mult)
+            nc.vector.tensor_copy(out=ms_words[:], in_=ms_bank[:, :, 0:PASSES])
+            nc.vector.tensor_tensor(out=b_terms[:], in0=b_terms[:], in1=qe_sb[:], op=ALU.mult)
+            qe_half = const.tile([P, PIX], BF16)
+            nc.vector.tensor_scalar(
+                out=qe_half[:], in0=qe_sb[:], scalar1=-0.5, scalar2=None, op0=ALU.mult
+            )
+
+            def sum_b():
+                b_bank = psum_sim.tile([P, PIX_TILES, P], F32, tag="u")
+                for pt in range(PIX_TILES):
+                    nc.tensor.transpose(
+                        b_bank[:, pt, :], b_terms[:, pt * P : (pt + 1) * P], ident_f32[:]
+                    )
+                b_sum = const.tile([P, PIX_TILES], F32)
+                nc.vector.reduce_sum(out=b_sum[:], in_=b_bank[:], axis=AXIS.X)
+                nc.vector.tensor_scalar(
+                    out=b_minus[:], in0=b_sum[:], scalar1=-0.5, scalar2=None, op0=ALU.mult
+                )
+
+            b_minus = const.tile([P, PIX_TILES], F32)
             ms_tiles = {}
 
             def spread_shrinkage(q):
@@ -290,6 +293,7 @@ def tile_xmem_pa_k_kernel(
                 )
 
             spread_shrinkage(0)
+            sum_b()
             for s in range(PASSES + LAG):
                 p = s - LAG
                 if s % 2 == 0 and s // 2 + 2 < PAIRS:
@@ -323,7 +327,7 @@ def tile_xmem_pa_k_kernel(
                     else:
                         empty_on_vector(0, s)
                 if p >= 0:
-                    if p < PASSES - LAG:
+                    if p < PASSES - 1:
                         empty_on_scalar(1, p)
                     else:
                         empty_on_vector(1, p)
@@ -336,23 +340,21 @@ def tile_xmem_pa_k_kernel(
 
                 if s % 2 == 0 and 2 <= s < PASSES:
                     maximum(0, s // 2 - 1)
-                if s % 2 == 1 and p >= 3:
-                    maximum(1, (p - 3) // 2)
                 if s == PASSES - 1:
                     maximum(0, PAIRS - 1)
                     find_shift(0)
+                if s % 2 == 1 and p >= 3:
+                    maximum(1, (p - 3) // 2)
 
             rest = EARLY_HALVES[len(HALF_STEPS) :] + [(0, 0), (0, 1), (1, 0), (1, 1)]
             for g in (0, 1):
                 mv_grouped[g] = wide_tile()
             for i in range(len(rest)):
                 transpose_values(*rest[i])
-                if i == 1:
-                    exponential(e0_pool, 0, 0, slice(0, PAIR), 0)
-                if i == 4:
-                    exponential(e0_pool, 0, 1, slice(0, PAIR), 1)
                 if i < len(rest) - VECTOR_REST:
                     copy_values(*rest[i], nc.scalar.copy)
+            for q in range(2):
+                exponential(e0_pool, 0, q, slice(0, PAIR), q)
             maximum(1, PAIRS - 1)
             find_shift(1)
             for i in range(len(rest) - VECTOR_REST, len(rest)):
@@ -389,9 +391,8 @@ def tile_xmem_pa_k_kernel(
 
             def copy_e(g):
                 e_four = e_grouped_pool.tile([P, PIX, 2], F32, align_bytes=64)
-                nc.vector.tensor_copy(
-                    out=e_four[:], in_=e_banks[g][:].rearrange("i u p -> i p u")
-                )
+                copy = nc.scalar.copy if g >= PASSES - SCALAR_LAST else nc.vector.tensor_copy
+                copy(out=e_four[:], in_=e_banks[g][:].rearrange("i u p -> i p u"))
                 e_grouped[g] = e_four
 
             def quantise(words, columns, pool):

@@ -26,7 +26,7 @@ PASSES = SLOTS // K_PASS
 PAIR = 2 * K_PASS
 PAIRS = SLOTS // PAIR
 VECTOR_REST = 4
-VSHARE = 4
+VSHARE = 2
 GSHARE = 4
 WARM_MATMULS = 3
 SCALAR_LAST = 3
@@ -120,12 +120,16 @@ def tile_xmem_pa_k_kernel(
         e_sums = const.tile([P, PIX_TILES, PAIRS + 1], F32)
         nc.vector.memset(e_sums[:, 0, PAIRS : PAIRS + 1], 0.0)
 
-        def exponential(pool, pt, q, cols, column):
+        def exponential(pool, pt, q, passes, column):
             if (pt, q) not in e_sb:
                 e_sb[(pt, q)] = pool.tile([P, PAIR], BF16, name="e")
+            slots = slice(passes.start * K_PASS, passes.stop * K_PASS)
+            columns = slice(passes.start * 2 * P, passes.stop * 2 * P)
             nc.scalar.activation(
-                out=e_sb[(pt, q)][:, cols],
-                in_=w[(pt, q)][:, cols],
+                out=e_sb[(pt, q)][:].rearrange("p (u x) -> p u x", u=2)[:, :, columns].rearrange(
+                    "p u (i e) -> p u i e", e=2
+                ),
+                in_=w[(pt, q)][:, slots].rearrange("p (i u e) -> p u i e", u=2, e=2),
                 func=ACT.Exp,
                 bias=shift[:, pt : pt + 1],
                 scale=EXP_SCALE,
@@ -139,24 +143,29 @@ def tile_xmem_pa_k_kernel(
 
             keys = {}
 
-            def load_keys(q):
-                slots = slice(q * PAIR, (q + 1) * PAIR)
+            def load_keys(q, pieces=1):
                 mk_sb = key_pool.tile([P, PAIR], BF16)
-                nc.sync.dma_start(out=mk_sb[:], in_=mk_dram[:, slots])
                 m2_sb = key_pool.tile([P, PAIR], BF16)
-                nc.sync.dma_start(out=m2_sb[:], in_=m2_dram[:, slots])
                 keys[q] = (mk_sb, m2_sb)
+                width = PAIR // pieces
+                for i in range(pieces):
+                    cols = slice(i * width, (i + 1) * width)
+                    slots = slice(q * PAIR + i * width, q * PAIR + (i + 1) * width)
+                    nc.sync.dma_start(out=mk_sb[:, cols], in_=mk_dram[:, slots])
+                    nc.sync.dma_start(out=m2_sb[:, cols], in_=m2_dram[:, slots])
 
+            zeros = e_grouped_pool.tile([P, K_PASS], BF16, tag="grouped", align_bytes=64)
+            nc.vector.memset(zeros[:].bitcast(F32), 0.0)
             ms_rows = const.tile([P, K_PASS], BF16)
-            nc.vector.memset(ms_rows[:].bitcast(F32), 0.0)
-            nc.sync.dma_start(out=ms_rows[0:PASSES, :], in_=ms_dram)
+            nc.gpsimd.memset(ms_rows[:].bitcast(F32), 0.0)
             qk_sb = const.tile([P, PIX], BF16)
             nc.sync.dma_start(out=qk_sb[:], in_=qk_dram)
             qe_sb = const.tile([P, PIX], BF16)
             nc.sync.dma_start(out=qe_sb[:], in_=qe_dram)
+            nc.sync.dma_start(out=ms_rows[0:PASSES, :], in_=ms_dram)
             qs_sb = const.tile([P, PIX], BF16)
             nc.sync.dma_start(out=qs_sb[:], in_=qs_dram)
-            load_keys(0)
+            load_keys(0, 2)
             load_keys(1)
 
             warm = const.tile([P, 1], F32)
@@ -165,8 +174,6 @@ def tile_xmem_pa_k_kernel(
             ident_f32 = const.tile([P, P], F32)
             make_identity(nc, ident_f32[:])
 
-            zeros = const.tile([P, K_PASS], BF16)
-            nc.vector.memset(zeros[:].bitcast(F32), 0.0)
             warm_bank = psum_sim.tile([P, K_PASS], F32, tag="u")
             for i in range(WARM_MATMULS):
                 nc.tensor.matmul(
@@ -182,8 +189,8 @@ def tile_xmem_pa_k_kernel(
 
             b_terms = const.tile([P, PIX], F32)
             nc.vector.tensor_tensor(out=b_terms[:], in0=qk_sb[:], in1=qk_sb[:], op=ALU.mult)
-            nc.vector.tensor_copy(out=ms_words[:], in_=ms_bank[:, :, 0:PASSES])
             nc.vector.tensor_tensor(out=b_terms[:], in0=b_terms[:], in1=qe_sb[:], op=ALU.mult)
+            nc.vector.tensor_copy(out=ms_words[:], in_=ms_bank[:, :, 0:PASSES])
             qe_half = const.tile([P, PIX], BF16)
             nc.vector.tensor_scalar(
                 out=qe_half[:], in0=qe_sb[:], scalar1=-0.5, scalar2=None, op0=ALU.mult
@@ -213,17 +220,13 @@ def tile_xmem_pa_k_kernel(
                             bank[:, s, u, :], column.to_broadcast([P, P]), ident_f32[:]
                         )
                 ms_sb = ms_pool.tile([P, PAIR], BF16)
-                nc.scalar.copy(
-                    out=ms_sb[:].bitcast(F32), in_=bank[:].rearrange("p s u i -> p (s u i)")
-                )
+                words = ms_sb[:].bitcast(F32).rearrange("p (s i u) -> p s i u", s=2, u=2)
+                nc.scalar.copy(out=words, in_=bank[:].rearrange("p s u i -> p s i u"))
                 ms_tiles[q] = ms_sb
 
             u_banks = {}
             pair_max = const.tile([P, PIX_TILES, PAIRS], F32)
             w_max = const.tile([P, PIX_TILES], F32)
-
-            def by_word(ap):
-                return ap.rearrange("p (i u e) -> p u i e", u=2, e=2)
 
             def pass_columns(s):
                 return slice((s % 2) * K_PASS, (s % 2 + 1) * K_PASS)
@@ -250,31 +253,29 @@ def tile_xmem_pa_k_kernel(
                 u_banks[(pt, s)] = u
 
             def empty_on_vector(pt, s):
-                for half in range(2):
-                    first = (s % 2) * K_PASS + half * 2 * P
-                    nc.vector.scalar_tensor_tensor(
-                        out=w[(pt, s // 2)][:, first : first + 2 * P].rearrange(
-                            "p (i e) -> p i e", e=2
-                        ),
-                        in0=by_word(u_banks[(pt, s)][:])[:, half],
-                        scalar=b_minus[:, pt : pt + 1],
-                        in1=ms_tiles[s // 2][:, first : first + 2 * P].rearrange(
-                            "p (i e) -> p i e", e=2
-                        ),
-                        op0=ALU.add,
-                        op1=ALU.mult,
-                    )
+                cols = pass_columns(s)
+                nc.vector.scalar_tensor_tensor(
+                    out=w[(pt, s // 2)][:, cols],
+                    in0=u_banks[(pt, s)][:],
+                    scalar=b_minus[:, pt : pt + 1],
+                    in1=ms_tiles[s // 2][:, cols],
+                    op0=ALU.add,
+                    op1=ALU.mult,
+                )
 
             def empty_on_scalar(pt, s):
                 w_cols = w[(pt, s // 2)][:, pass_columns(s)]
                 nc.scalar.activation(
-                    out=w_cols.rearrange("p (u i e) -> p u i e", u=2, e=2),
-                    in_=by_word(u_banks[(pt, s)][:]),
+                    out=w_cols,
+                    in_=u_banks[(pt, s)][:],
                     func=ACT.Identity,
                     bias=b_minus[:, pt : pt + 1],
                 )
+
+            def scale_on_gpsimd(pt, q, cols):
+                w_cols = w[(pt, q)][:, cols]
                 nc.gpsimd.tensor_tensor(
-                    out=w_cols, in0=w_cols, in1=ms_tiles[s // 2][:, pass_columns(s)], op=ALU.mult
+                    out=w_cols, in0=w_cols, in1=ms_tiles[q][:, cols], op=ALU.mult
                 )
 
             def maximum(pt, q):
@@ -324,11 +325,16 @@ def tile_xmem_pa_k_kernel(
                 if s < PASSES:
                     if s % GSHARE == 2 and s < PASSES - 4:
                         empty_on_scalar(0, s)
+                        scale_on_gpsimd(0, s // 2, pass_columns(s))
                     else:
                         empty_on_vector(0, s)
                 if p >= 0:
                     if p < PASSES - 1:
                         empty_on_scalar(1, p)
+                        if p == PASSES - 2:
+                            scale_on_gpsimd(1, p // 2, pass_columns(p))
+                        elif p % 2 == 1:
+                            scale_on_gpsimd(1, p // 2, slice(0, PAIR))
                     else:
                         empty_on_vector(1, p)
                 if s % 2 == 0 and s // 2 + 1 < PAIRS:
@@ -354,7 +360,7 @@ def tile_xmem_pa_k_kernel(
                 if i < len(rest) - VECTOR_REST:
                     copy_values(*rest[i], nc.scalar.copy)
             for q in range(2):
-                exponential(e0_pool, 0, q, slice(0, PAIR), q)
+                exponential(e0_pool, 0, q, slice(0, 2), q)
             maximum(1, PAIRS - 1)
             find_shift(1)
             for i in range(len(rest) - VECTOR_REST, len(rest)):
@@ -381,7 +387,7 @@ def tile_xmem_pa_k_kernel(
                 for pt in range(PIX_TILES):
                     words = e_sb[(pt, q)][:].bitcast(F32)
                     for u in range(2):
-                        first = s * (K_PASS // 2) + u * P
+                        first = (2 * u + s) * P
                         nc.tensor.transpose(
                             bank[:, u, pt * P : (pt + 1) * P],
                             words[:, first : first + P],
@@ -390,7 +396,7 @@ def tile_xmem_pa_k_kernel(
                 e_banks[g] = bank
 
             def copy_e(g):
-                e_four = e_grouped_pool.tile([P, PIX, 2], F32, align_bytes=64)
+                e_four = e_grouped_pool.tile([P, PIX, 2], F32, tag="grouped", align_bytes=64)
                 copy = nc.scalar.copy if g >= PASSES - SCALAR_LAST else nc.vector.tensor_copy
                 copy(out=e_four[:], in_=e_banks[g][:].rearrange("i u p -> i p u"))
                 e_grouped[g] = e_four
@@ -416,8 +422,8 @@ def tile_xmem_pa_k_kernel(
                         stop=(g == PASSES - 1),
                     )
 
-            exponential(e1_pool, 1, 0, slice(0, K_PASS), 0)
-            exponential(e1_pool, 1, 0, slice(K_PASS, PAIR), PAIRS)
+            exponential(e1_pool, 1, 0, slice(0, 1), 0)
+            exponential(e1_pool, 1, 0, slice(1, 2), PAIRS)
             for g in LATE[2:6]:
                 load_values(g)
             halves = {k: [(k + 2, 0), (k + 2, 1)] for k in range(2)}
@@ -444,7 +450,7 @@ def tile_xmem_pa_k_kernel(
                         copy_values(g, h, nc.scalar.copy)
                 if (k + 3) // 2 < PAIRS:
                     pt = (k + 1) % 2
-                    exponential(e_pools[pt], pt, (k + 3) // 2, slice(0, PAIR), (k + 3) // 2)
+                    exponential(e_pools[pt], pt, (k + 3) // 2, slice(0, 2), (k + 3) // 2)
 
                 if 1 <= k <= PASSES:
                     copy_e(k - 1)

@@ -21,6 +21,7 @@ SLOTS = 16384
 VAL = 512
 VAL_TILES = VAL // P
 HALF_VAL = VAL // 2
+HALF_TILES = HALF_VAL // P
 K_PASS = 4 * P
 PASSES = SLOTS // K_PASS
 PAIR = 2 * K_PASS
@@ -33,11 +34,16 @@ SCALAR_LAST = 3
 LAG = 2
 EXP_SCALE = 2.0 / math.sqrt(CK)
 
-EARLY = list(range(6, PASSES, 2))
-EARLY_HALVES = [(g, h) for g in EARLY for h in range(2)]
+EARLY_PAIRS = [3, 5, 7, 9, 11, 13, 15]
+LATE_PAIRS = [m for m in range(PAIRS) if m not in EARLY_PAIRS]
+EARLY = [2 * m + s for m in EARLY_PAIRS for s in range(2)]
+UNITS = [(m, h) for m in EARLY_PAIRS + LATE_PAIRS for h in range(2)]
+EARLY_HALVES = [(2 * m + s, h) for m in EARLY_PAIRS for h in range(2) for s in range(2)]
+LATE_HALVES = [(2 * m + s, h) for m in LATE_PAIRS for h in range(2) for s in range(2)]
 FIRST_EARLY = 3
-HALF_STEPS = [s for s in range(FIRST_EARLY, PASSES) if s % 4 != 2]
-LATE = [g for g in range(PASSES) if g not in EARLY]
+HALF_STEPS = [s for s in range(FIRST_EARLY, PASSES) if s % 8 != 3]
+IN_PHASE_1 = (len(HALF_STEPS) + 1) // 2
+RAW = 4
 
 FLOPS = 2 * SLOTS * PIX * (2 * CK + VAL)
 
@@ -73,8 +79,8 @@ def tile_xmem_pa_k_kernel(
         const = whole.enter_context(tc.tile_pool(name="const", bufs=1))
         wide_pool = whole.enter_context(tc.tile_pool(name="wide", bufs=PIX_TILES * PAIRS))
         early_pool = whole.enter_context(tc.tile_pool(name="early", bufs=1))
-        raw_pool = whole.enter_context(tc.tile_pool(name="raw", bufs=4))
-        e_grouped_pool = whole.enter_context(tc.tile_pool(name="e_grouped", bufs=3))
+        raw_pool = whole.enter_context(tc.tile_pool(name="raw", bufs=RAW))
+        e_grouped_pool = whole.enter_context(tc.tile_pool(name="e_grouped", bufs=2))
         e0_pool = whole.enter_context(tc.tile_pool(name="e0", bufs=3))
         psum_val = whole.enter_context(tc.psum_pool(name="psum_val", bufs=4))
 
@@ -82,19 +88,31 @@ def tile_xmem_pa_k_kernel(
         mv_banks = {}
         mv_grouped = {}
 
-        def load_values(g):
-            raw = raw_pool.tile([P, VAL_TILES, K_PASS], BF16)
-            nc.sync.dma_start(out=raw[:], in_=mv_dram[:, :, g * K_PASS : (g + 1) * K_PASS])
-            raws[g] = raw
+        def load_values(i):
+            if i < len(UNITS):
+                m, h = UNITS[i]
+                raw = raw_pool.tile([P, HALF_TILES, PAIR], BF16)
+                nc.sync.dma_start(
+                    out=raw[:],
+                    in_=mv_dram[
+                        :, h * HALF_TILES : (h + 1) * HALF_TILES, m * PAIR : (m + 1) * PAIR
+                    ],
+                )
+                raws[(m, h)] = raw
+
+        def load_behind(g, h):
+            if g % 2 == 1:
+                load_values(UNITS.index((g // 2, h)) + RAW)
 
         def transpose_values(g, h):
             bank = psum_val.tile([P, 2, HALF_VAL], F32, tag="val")
             for u in range(2):
-                for q in range(HALF_VAL // P):
-                    words = raws[g][:, h * (HALF_VAL // P) + q, :].bitcast(F32)
+                for q in range(HALF_TILES):
+                    words = raws[(g // 2, h)][:, q, :].bitcast(F32)
+                    first = (g % 2) * (K_PASS // 2) + u
                     nc.tensor.transpose(
                         bank[:, u, q * P : (q + 1) * P],
-                        words[:, u : 2 * P : 2],
+                        words[:, first : first + 2 * P - 1 : 2],
                         ident_f32[:],
                     )
             mv_banks[(g, h)] = bank
@@ -156,7 +174,7 @@ def tile_xmem_pa_k_kernel(
 
             zeros = e_grouped_pool.tile([P, K_PASS], BF16, tag="grouped", align_bytes=64)
             nc.vector.memset(zeros[:].bitcast(F32), 0.0)
-            ms_rows = const.tile([P, K_PASS], BF16)
+            ms_rows = e0_pool.tile([P, K_PASS], BF16, name="e")
             nc.gpsimd.memset(ms_rows[:].bitcast(F32), 0.0)
             qk_sb = const.tile([P, PIX], BF16)
             nc.sync.dma_start(out=qk_sb[:], in_=qk_dram)
@@ -187,7 +205,7 @@ def tile_xmem_pa_k_kernel(
                 )
             ms_words = const.tile([P, 2, PASSES], F32)
 
-            b_terms = const.tile([P, PIX], F32)
+            b_terms = e_grouped_pool.tile([P, PIX], F32, tag="grouped", align_bytes=64)
             nc.vector.tensor_tensor(out=b_terms[:], in0=qk_sb[:], in1=qk_sb[:], op=ALU.mult)
             nc.vector.tensor_tensor(out=b_terms[:], in0=b_terms[:], in1=qe_sb[:], op=ALU.mult)
             nc.vector.tensor_copy(out=ms_words[:], in_=ms_bank[:, :, 0:PASSES])
@@ -293,23 +311,18 @@ def tile_xmem_pa_k_kernel(
                     op0=ALU.mult,
                 )
 
-            spread_shrinkage(0)
             sum_b()
+            spread_shrinkage(0)
             for s in range(PASSES + LAG):
                 p = s - LAG
                 if s % 2 == 0 and s // 2 + 2 < PAIRS:
                     load_keys(s // 2 + 2)
-                for step in HALF_STEPS:
-                    g, h = EARLY_HALVES[HALF_STEPS.index(step)]
-                    if h == 0 and s == max(0, step - 5):
-                        load_values(g)
-                if s == PASSES - 1:
-                    for g, h in EARLY_HALVES[len(HALF_STEPS) :]:
-                        if h == 0:
-                            load_values(g)
-                if s == PASSES:
-                    load_values(0)
-                    load_values(1)
+                for i in range(IN_PHASE_1):
+                    if s == max(0, HALF_STEPS[2 * i] - 6):
+                        load_values(i)
+                for i in range(IN_PHASE_1, len(HALF_STEPS) // 2 + RAW):
+                    if s == PASSES - 5 + 2 * (i - IN_PHASE_1):
+                        load_values(i)
 
                 if s % 2 == 0:
                     if s < PASSES:
@@ -352,18 +365,21 @@ def tile_xmem_pa_k_kernel(
                 if s % 2 == 1 and p >= 3:
                     maximum(1, (p - 3) // 2)
 
-            rest = EARLY_HALVES[len(HALF_STEPS) :] + [(0, 0), (0, 1), (1, 0), (1, 1)]
+            rest = EARLY_HALVES[len(HALF_STEPS) :] + LATE_HALVES[:4]
             for g in (0, 1):
                 mv_grouped[g] = wide_tile()
             for i in range(len(rest)):
                 transpose_values(*rest[i])
+                load_behind(*rest[i])
                 if i < len(rest) - VECTOR_REST:
                     copy_values(*rest[i], nc.scalar.copy)
             for q in range(2):
                 exponential(e0_pool, 0, q, slice(0, 2), q)
+            for i in range(len(rest) - VECTOR_REST, len(rest) - VECTOR_REST + 2):
+                copy_values(*rest[i], nc.scalar.copy)
             maximum(1, PAIRS - 1)
             find_shift(1)
-            for i in range(len(rest) - VECTOR_REST, len(rest)):
+            for i in range(len(rest) - VECTOR_REST + 2, len(rest)):
                 copy_values(*rest[i], nc.vector.tensor_copy)
 
         psum_acc = whole.enter_context(tc.psum_pool(name="psum_acc", bufs=1))
@@ -424,22 +440,18 @@ def tile_xmem_pa_k_kernel(
 
             exponential(e1_pool, 1, 0, slice(0, 1), 0)
             exponential(e1_pool, 1, 0, slice(1, 2), PAIRS)
-            for g in LATE[2:6]:
-                load_values(g)
-            halves = {k: [(k + 2, 0), (k + 2, 1)] for k in range(2)}
-            for g in LATE[4:]:
-                for h in range(2):
-                    halves[g - 3 + h] = halves.get(g - 3 + h, []) + [(g, h)]
-            on_vector = [(g, 1) for g in LATE if LATE.index(g) % VSHARE == 0]
-            loads = LATE[6:]
+            halves = {}
+            for j in range(4, len(LATE_HALVES)):
+                g, h = LATE_HALVES[j]
+                step = [0, 0, 0, 1, 1, 2, 2, 3][j - 4] if j < 12 else 2 * (g // 2) - 4 + j % 4
+                halves[step] = halves.get(step, []) + [(g, h)]
+            on_vector = LATE_HALVES[0::4]
             for k in range(PASSES + 3):
-                if loads and k + 7 >= loads[0]:
-                    load_values(loads[0])
-                    loads = loads[1:]
                 if k < PASSES:
                     transpose_e(k)
                 for half in halves.get(k, []):
                     transpose_values(*half)
+                    load_behind(*half)
                 if k >= 3:
                     readout(k - 3)
 

import math
from contextlib import ExitStack

import concourse.mybir as mybir
from concourse.masks import make_identity

F32 = mybir.dt.float32
BF16 = mybir.dt.bfloat16
U32 = mybir.dt.uint32
U8 = mybir.dt.uint8
FP8X4 = mybir.dt.float8_e4m3fn_x4
ALU = mybir.AluOpType
ACT = mybir.ActivationFunctionType
AXIS = mybir.AxisListType

P = 128
CK = 128
PIX = 256
PIX_TILES = PIX // P
SLOTS = 16384
VAL = 512
VAL_TILES = VAL // P
HALF_VAL = VAL // 2
HALF_TILES = HALF_VAL // P
K_PASS = 4 * P
PASSES = SLOTS // K_PASS
PAIR = 2 * K_PASS
PAIRS = SLOTS // PAIR
VECTOR_REST = 4
VSHARE = 2
GSHARE = 4
WARM_MATMULS = 3
SCALAR_LAST = 3
LAG = 2
EXP_SCALE = 2.0 / math.sqrt(CK)

EARLY_PAIRS = [3, 5, 7, 9, 11, 13, 15]
LATE_PAIRS = [m for m in range(PAIRS) if m not in EARLY_PAIRS]
EARLY = [2 * m + s for m in EARLY_PAIRS for s in range(2)]
UNITS = [(m, h) for m in EARLY_PAIRS + LATE_PAIRS for h in range(2)]
EARLY_HALVES = [(2 * m + s, h) for m in EARLY_PAIRS for h in range(2) for s in range(2)]
LATE_HALVES = [(2 * m + s, h) for m in LATE_PAIRS for h in range(2) for s in range(2)]
FIRST_EARLY = 3
HALF_STEPS = [s for s in range(FIRST_EARLY, PASSES) if s % 8 != 3]
IN_PHASE_1 = (len(HALF_STEPS) + 1) // 2
RAW = 4

FLOPS = 2 * SLOTS * PIX * (2 * CK + VAL)


def tile_xmem_pa_k_kernel(
    tc,
    query_key,
    query_selection,
    qk_sel,
    memory_key,
    mk_sq,
    memory_shrinkage,
    memory_value,
    out,
):
    nc = tc.nc

    qk_dram = query_key.rearrange("b c h w -> (b c) (h w)")
    qe_dram = query_selection.rearrange("b c h w -> (b c) (h w)")
    qs_dram = qk_sel.rearrange("b c h w -> (b c) (h w)")
    mk_dram = memory_key.rearrange("b c t h w -> (b c) (t h w)")
    m2_dram = mk_sq.rearrange("b c t h w -> (b c) (t h w)")
    ms_dram = memory_shrinkage.rearrange("b o t h w -> (b o t h w)").rearrange(
        "(s n) -> s n", s=PASSES
    )
    mv_dram = memory_value.rearrange("b o c t h w -> (b o c) (t h w)").rearrange(
        "(q r) n -> r q n", r=P
    )
    out_dram = out.rearrange("b o c h w -> (b o c) (h w)").rearrange("(q r) p -> r q p", r=P)

    with ExitStack() as whole:
        whole.enter_context(tc.manual_schedule())
        const = whole.enter_context(tc.tile_pool(name="const", bufs=1))
        wide_pool = whole.enter_context(tc.tile_pool(name="wide", bufs=PIX_TILES * PAIRS))
        early_pool = whole.enter_context(tc.tile_pool(name="early", bufs=1))
        raw_pool = whole.enter_context(tc.tile_pool(name="raw", bufs=RAW))
        e_grouped_pool = whole.enter_context(tc.tile_pool(name="e_grouped", bufs=2))
        e0_pool = whole.enter_context(tc.tile_pool(name="e0", bufs=3))
        psum_val = whole.enter_context(tc.psum_pool(name="psum_val", bufs=4))

        raws = {}
        mv_banks = {}
        mv_grouped = {}

        def load_values(i):
            if i < len(UNITS):
                m, h = UNITS[i]
                raw = raw_pool.tile([P, HALF_TILES, PAIR], BF16)
                nc.sync.dma_start(
                    out=raw[:],
                    in_=mv_dram[
                        :, h * HALF_TILES : (h + 1) * HALF_TILES, m * PAIR : (m + 1) * PAIR
                    ],
                )
                raws[(m, h)] = raw

        def load_behind(g, h):
            if g % 2 == 1:
                load_values(UNITS.index((g // 2, h)) + RAW)

        def transpose_values(g, h):
            bank = psum_val.tile([P, 2, HALF_VAL], F32, tag="val")
            for u in range(2):
                for q in range(HALF_TILES):
                    words = raws[(g // 2, h)][:, q, :].bitcast(F32)
                    first = (g % 2) * (K_PASS // 2) + u
                    nc.tensor.transpose(
                        bank[:, u, q * P : (q + 1) * P],
                        words[:, first : first + 2 * P - 1 : 2],
                        ident_f32[:],
                    )
            mv_banks[(g, h)] = bank

        def copy_values(g, h, copy):
            pairs = mv_grouped[g][:].rearrange("i (v u) -> i v u", u=2)
            copy(
                out=pairs[:, h * HALF_VAL : (h + 1) * HALF_VAL, :],
                in_=mv_banks[(g, h)][:].rearrange("i u v -> i v u"),
            )

        w = {}

        def wide_tile():
            tile = wide_pool.tile([P, PAIR], F32, tag="wide", align_bytes=64)
            return tile

        for g in EARLY:
            mv_grouped[g] = early_pool.tile([P, 2 * VAL], F32, name="early%d" % g, align_bytes=64)

        e_sb = {}
        shift = const.tile([P, PIX_TILES], F32)
        e_sums = const.tile([P, PIX_TILES, PAIRS + 1], F32)
        nc.vector.memset(e_sums[:, 0, PAIRS : PAIRS + 1], 0.0)

        def exponential(pool, pt, q, passes, column):
            if (pt, q) not in e_sb:
                e_sb[(pt, q)] = pool.tile([P, PAIR], BF16, name="e")
            slots = slice(passes.start * K_PASS, passes.stop * K_PASS)
            columns = slice(passes.start * 2 * P, passes.stop * 2 * P)
            nc.scalar.activation(
                out=e_sb[(pt, q)][:].rearrange("p (u x) -> p u x", u=2)[:, :, columns].rearrange(
                    "p u (i e) -> p u i e", e=2
                ),
                in_=w[(pt, q)][:, slots].rearrange("p (i u e) -> p u i e", u=2, e=2),
                func=ACT.Exp,
                bias=shift[:, pt : pt + 1],
                scale=EXP_SCALE,
                accum_out=e_sums[:, pt, column : column + 1],
            )

        with ExitStack() as phase1:
            key_pool = phase1.enter_context(tc.tile_pool(name="keys", bufs=4))
            ms_pool = phase1.enter_context(tc.tile_pool(name="ms", bufs=4))
            psum_sim = phase1.enter_context(tc.psum_pool(name="psum_sim", bufs=4))

            keys = {}

            def load_keys(q, pieces=1):
                mk_sb = key_pool.tile([P, PAIR], BF16)
                m2_sb = key_pool.tile([P, PAIR], BF16)
                keys[q] = (mk_sb, m2_sb)
                width = PAIR // pieces
                for i in range(pieces):
                    cols = slice(i * width, (i + 1) * width)
                    slots = slice(q * PAIR + i * width, q * PAIR + (i + 1) * width)
                    nc.sync.dma_start(out=mk_sb[:, cols], in_=mk_dram[:, slots])
                    nc.sync.dma_start(out=m2_sb[:, cols], in_=m2_dram[:, slots])

            zeros = e_grouped_pool.tile([P, K_PASS], BF16, tag="grouped", align_bytes=64)
            nc.vector.memset(zeros[:].bitcast(F32), 0.0)
            ms_rows = e0_pool.tile([P, K_PASS], BF16, name="e")
            nc.gpsimd.memset(ms_rows[:].bitcast(F32), 0.0)
            qk_sb = const.tile([P, PIX], BF16)
            nc.sync.dma_start(out=qk_sb[:], in_=qk_dram)
            qe_sb = const.tile([P, PIX], BF16)
            nc.sync.dma_start(out=qe_sb[:], in_=qe_dram)
            nc.sync.dma_start(out=ms_rows[0:PASSES, :], in_=ms_dram)
            qs_sb = const.tile([P, PIX], BF16)
            nc.sync.dma_start(out=qs_sb[:], in_=qs_dram)
            load_keys(0, 2)
            load_keys(1)

            warm = const.tile([P, 1], F32)
            nc.vector.memset(warm[:], 0.0)
            nc.scalar.activation(out=warm[:], in_=warm[:], func=ACT.Exp)
            ident_f32 = const.tile([P, P], F32)
            make_identity(nc, ident_f32[:])

            warm_bank = psum_sim.tile([P, K_PASS], F32, tag="u")
            for i in range(WARM_MATMULS):
                nc.tensor.matmul(
                    warm_bank[:], lhsT=zeros[:, 0:P], rhs=zeros[:], start=True, stop=True
                )

            ms_bank = psum_val.tile([P, 2, P], F32, tag="val")
            for u in range(2):
                nc.tensor.transpose(
                    ms_bank[:, u, :], ms_rows[:].bitcast(F32)[:, u::2], ident_f32[:]
                )
            ms_words = const.tile([P, 2, PASSES], F32)

            b_terms = e_grouped_pool.tile([P, PIX], F32, tag="grouped", align_bytes=64)
            nc.vector.tensor_tensor(out=b_terms[:], in0=qk_sb[:], in1=qk_sb[:], op=ALU.mult)
            nc.vector.tensor_tensor(out=b_terms[:], in0=b_terms[:], in1=qe_sb[:], op=ALU.mult)
            nc.vector.tensor_copy(out=ms_words[:], in_=ms_bank[:, :, 0:PASSES])
            qe_half = const.tile([P, PIX], BF16)
            nc.vector.tensor_scalar(
                out=qe_half[:], in0=qe_sb[:], scalar1=-0.5, scalar2=None, op0=ALU.mult
            )

            def sum_b():
                b_bank = psum_sim.tile([P, PIX_TILES, P], F32, tag="u")
                for pt in range(PIX_TILES):
                    nc.tensor.transpose(
                        b_bank[:, pt, :], b_terms[:, pt * P : (pt + 1) * P], ident_f32[:]
                    )
                b_sum = const.tile([P, PIX_TILES], F32)
                nc.vector.reduce_sum(out=b_sum[:], in_=b_bank[:], axis=AXIS.X)
                nc.vector.tensor_scalar(
                    out=b_minus[:], in0=b_sum[:], scalar1=-0.5, scalar2=None, op0=ALU.mult
                )

            b_minus = const.tile([P, PIX_TILES], F32)
            ms_tiles = {}

            def spread_shrinkage(q):
                bank = psum_val.tile([P, 2, 2, P], F32, tag="val")
                for s in range(2):
                    for u in range(2):
                        column = ms_words[:, u, 2 * q + s : 2 * q + s + 1]
                        nc.tensor.transpose(
                            bank[:, s, u, :], column.to_broadcast([P, P]), ident_f32[:]
                        )
                ms_sb = ms_pool.tile([P, PAIR], BF16)
                words = ms_sb[:].bitcast(F32).rearrange("p (s i u) -> p s i u", s=2, u=2)
                nc.scalar.copy(out=words, in_=bank[:].rearrange("p s u i -> p s i u"))
                ms_tiles[q] = ms_sb

            u_banks = {}
            pair_max = const.tile([P, PIX_TILES, PAIRS], F32)
            w_max = const.tile([P, PIX_TILES], F32)

            def pass_columns(s):
                return slice((s % 2) * K_PASS, (s % 2 + 1) * K_PASS)

            def similarities(pt, s):
                mk_sb, m2_sb = keys[s // 2]
                cols = pass_columns(s)
                pixels = slice(pt * P, (pt + 1) * P)
                u = psum_sim.tile([P, K_PASS], F32, tag="u")
                nc.tensor.matmul(
                    u[:],
                    lhsT=qs_sb[:, pixels],
                    rhs=mk_sb[:, cols],
                    start=True,
                    stop=False,
                )
                nc.tensor.matmul(
                    u[:],
                    lhsT=qe_half[:, pixels],
                    rhs=m2_sb[:, cols],
                    start=False,
                    stop=True,
                )
                u_banks[(pt, s)] = u

            def empty_on_vector(pt, s):
                cols = pass_columns(s)
                nc.vector.scalar_tensor_tensor(
                    out=w[(pt, s // 2)][:, cols],
                    in0=u_banks[(pt, s)][:],
                    scalar=b_minus[:, pt : pt + 1],
                    in1=ms_tiles[s // 2][:, cols],
                    op0=ALU.add,
                    op1=ALU.mult,
                )

            def empty_on_scalar(pt, s):
                w_cols = w[(pt, s // 2)][:, pass_columns(s)]
                nc.scalar.activation(
                    out=w_cols,
                    in_=u_banks[(pt, s)][:],
                    func=ACT.Identity,
                    bias=b_minus[:, pt : pt + 1],
                )

            def scale_on_gpsimd(pt, q, cols):
                w_cols = w[(pt, q)][:, cols]
                nc.gpsimd.tensor_tensor(
                    out=w_cols, in0=w_cols, in1=ms_tiles[q][:, cols], op=ALU.mult
                )

            def maximum(pt, q):
                nc.vector.reduce_max(out=pair_max[:, pt, q : q + 1], in_=w[(pt, q)][:], axis=AXIS.X)

            def find_shift(pt):
                nc.vector.reduce_max(
                    out=w_max[:, pt : pt + 1], in_=pair_max[:, pt, :], axis=AXIS.X
                )
                nc.vector.tensor_scalar(
                    out=shift[:, pt : pt + 1],
                    in0=w_max[:, pt : pt + 1],
                    scalar1=-EXP_SCALE,
                    scalar2=None,
                    op0=ALU.mult,
                )

            sum_b()
            spread_shrinkage(0)
            for s in range(PASSES + LAG):
                p = s - LAG
                if s % 2 == 0 and s // 2 + 2 < PAIRS:
                    load_keys(s // 2 + 2)
                for i in range(IN_PHASE_1):
                    if s == max(0, HALF_STEPS[2 * i] - 6):
                        load_values(i)
                for i in range(IN_PHASE_1, len(HALF_STEPS) // 2 + RAW):
                    if s == PASSES - 5 + 2 * (i - IN_PHASE_1):
                        load_values(i)

                if s % 2 == 0:
                    if s < PASSES:
                        w[(0, s // 2)] = wide_tile()
                    if p >= 0:
                        w[(1, p // 2)] = wide_tile()

                if s < PASSES:
                    similarities(0, s)
                if p >= 0:
                    similarities(1, p)

                if s < PASSES:
                    if s % GSHARE == 2 and s < PASSES - 4:
                        empty_on_scalar(0, s)
                        scale_on_gpsimd(0, s // 2, pass_columns(s))
                    else:
                        empty_on_vector(0, s)
                if p >= 0:
                    if p < PASSES - 1:
                        empty_on_scalar(1, p)
                        if p == PASSES - 2:
                            scale_on_gpsimd(1, p // 2, pass_columns(p))
                        elif p % 2 == 1:
                            scale_on_gpsimd(1, p // 2, slice(0, PAIR))
                    else:
                        empty_on_vector(1, p)
                if s % 2 == 0 and s // 2 + 1 < PAIRS:
                    spread_shrinkage(s // 2 + 1)
                if s - 1 in HALF_STEPS:
                    copy_values(*EARLY_HALVES[HALF_STEPS.index(s - 1)], nc.scalar.copy)
                if s in HALF_STEPS:
                    transpose_values(*EARLY_HALVES[HALF_STEPS.index(s)])

                if s % 2 == 0 and 2 <= s < PASSES:
                    maximum(0, s // 2 - 1)
                if s == PASSES - 1:
                    maximum(0, PAIRS - 1)
                    find_shift(0)
                if s % 2 == 1 and p >= 3:
                    maximum(1, (p - 3) // 2)

            rest = EARLY_HALVES[len(HALF_STEPS) :] + LATE_HALVES[:4]
            for g in (0, 1):
                mv_grouped[g] = wide_tile()
            for i in range(len(rest)):
                transpose_values(*rest[i])
                load_behind(*rest[i])
                if i < len(rest) - VECTOR_REST:
                    copy_values(*rest[i], nc.scalar.copy)
            for q in range(2):
                exponential(e0_pool, 0, q, slice(0, 2), q)
            for i in range(len(rest) - VECTOR_REST, len(rest) - VECTOR_REST + 2):
                copy_values(*rest[i], nc.scalar.copy)
            maximum(1, PAIRS - 1)
            find_shift(1)
            for i in range(len(rest) - VECTOR_REST + 2, len(rest)):
                copy_values(*rest[i], nc.vector.tensor_copy)

        psum_acc = whole.enter_context(tc.psum_pool(name="psum_acc", bufs=1))
        acc = [psum_acc.tile([P, VAL], F32, name="acc%d" % pt) for pt in range(PIX_TILES)]

        with ExitStack() as phase:
            e1_pool = phase.enter_context(tc.tile_pool(name="e1", bufs=3))
            e_mx_pool = phase.enter_context(tc.tile_pool(name="e_mx", bufs=4))
            mv_mx_pool = phase.enter_context(tc.tile_pool(name="mv_mx", bufs=5))
            psum_e = phase.enter_context(tc.psum_pool(name="psum_e", bufs=2))
            e_pools = [e0_pool, e1_pool]

            e_banks = {}
            e_grouped = {}
            e_codes = {}
            mv_codes = {}

            def transpose_e(g):
                q, s = divmod(g, 2)
                bank = psum_e.tile([P, 2, PIX], F32)
                for pt in range(PIX_TILES):
                    words = e_sb[(pt, q)][:].bitcast(F32)
                    for u in range(2):
                        first = (2 * u + s) * P
                        nc.tensor.transpose(
                            bank[:, u, pt * P : (pt + 1) * P],
                            words[:, first : first + P],
                            ident_f32[:],
                        )
                e_banks[g] = bank

            def copy_e(g):
                e_four = e_grouped_pool.tile([P, PIX, 2], F32, tag="grouped", align_bytes=64)
                copy = nc.scalar.copy if g >= PASSES - SCALAR_LAST else nc.vector.tensor_copy
                copy(out=e_four[:], in_=e_banks[g][:].rearrange("i u p -> i p u"))
                e_grouped[g] = e_four

            def quantise(words, columns, pool):
                codes = pool.tile([P, columns], U32, align_bytes=256)
                scales = pool.tile([P, columns], U8, align_bytes=256)
                nc.vector.quantize_mx(
                    out=codes[:].bitcast(FP8X4), scales=scales[:], in_=words.bitcast(BF16)
                )
                return codes, scales

            def readout(g):
                for pt in range(PIX_TILES):
                    pixels = slice(pt * P, (pt + 1) * P)
                    nc.tensor.matmul_mx(
                        out=acc[pt][:],
                        lhsT=e_codes[g][0][:, pixels].bitcast(FP8X4),
                        lhsT_scale=e_codes[g][1][:, pixels],
                        rhs=mv_codes[g][0][:].bitcast(FP8X4),
                        rhs_scale=mv_codes[g][1][:],
                        start=(g == 0),
                        stop=(g == PASSES - 1),
                    )

            exponential(e1_pool, 1, 0, slice(0, 1), 0)
            exponential(e1_pool, 1, 0, slice(1, 2), PAIRS)
            halves = {}
            for j in range(4, len(LATE_HALVES)):
                g, h = LATE_HALVES[j]
                step = [0, 0, 0, 1, 1, 2, 2, 3][j - 4] if j < 12 else 2 * (g // 2) - 4 + j % 4
                halves[step] = halves.get(step, []) + [(g, h)]
            on_vector = LATE_HALVES[0::4]
            for k in range(PASSES + 3):
                if k < PASSES:
                    transpose_e(k)
                for half in halves.get(k, []):
                    transpose_values(*half)
                    load_behind(*half)
                if k >= 3:
                    readout(k - 3)

                for g, h in halves.get(k - 1, []):
                    if h == 0:
                        mv_grouped[g] = wide_tile()
                    if (g, h) not in on_vector:
                        copy_values(g, h, nc.scalar.copy)
                if (k + 3) // 2 < PAIRS:
                    pt = (k + 1) % 2
                    exponential(e_pools[pt], pt, (k + 3) // 2, slice(0, 2), (k + 3) // 2)

                if 1 <= k <= PASSES:
                    copy_e(k - 1)
                for half in halves.get(k - 1, []):
                    if half in on_vector:
                        copy_values(*half, nc.vector.tensor_copy)
                if 2 <= k <= PASSES + 1:
                    e_codes[k - 2] = quantise(
                        e_grouped[k - 2][:].rearrange("i p u -> i (p u)"), PIX, e_mx_pool
                    )
                if k < PASSES:
                    mv_codes[k] = quantise(mv_grouped[k][:], VAL, mv_mx_pool)

        with tc.tile_pool(name="tail", bufs=VAL_TILES) as tail:
            result_banks = []
            total = const.tile([P, PIX_TILES], F32)
            nc.vector.reduce_sum(out=total[:], in_=e_sums[:], axis=AXIS.X)
            inv_total = const.tile([P, PIX_TILES], F32)
            nc.vector.reciprocal(out=inv_total[:], in_=total[:])

            for c in range(VAL_TILES):
                channels = slice(c * P, (c + 1) * P)
                mem0 = tail.tile([P, P], F32)
                nc.vector.tensor_scalar(
                    out=mem0[:],
                    in0=acc[0][:, channels],
                    scalar1=inv_total[:, 0:1],
                    scalar2=None,
                    op0=ALU.mult,
                )
                mem1 = tail.tile([P, P], F32)
                nc.scalar.activation(
                    out=mem1[:], in_=acc[1][:, channels], func=ACT.Copy, scale=inv_total[:, 1:2]
                )
                bank = psum_val.tile([P, PIX], F32, tag="val")
                nc.tensor.transpose(bank[:, 0:P], mem0[:], ident_f32[:])
                nc.tensor.transpose(bank[:, P:PIX], mem1[:], ident_f32[:])
                result_banks.append(bank)
            for c in range(VAL_TILES):
                result = tail.tile([P, PIX], F32)
                if c % 2 == 0:
                    nc.vector.tensor_copy(out=result[:], in_=result_banks[c][:])
                else:
                    nc.scalar.copy(out=result[:], in_=result_banks[c][:])
                nc.sync.dma_start(out=out_dram[:, c, :], in_=result[:])
